import numpy as np
import ml_dtypes


def mxq(x, axis, fmt="e4m3"):
    dtype, down = {"e4m3": (ml_dtypes.float8_e4m3fn, 7), "e5m2": (ml_dtypes.float8_e5m2, 14)}[fmt]
    v = np.moveaxis(np.asarray(x, np.float32).astype(ml_dtypes.bfloat16).astype(np.float64), axis, -1)
    blocks = v.reshape(v.shape[:-1] + (-1, 32))
    amax = np.abs(blocks).max(-1, keepdims=True)
    byte = np.maximum(np.where(amax > 0, np.frexp(amax)[1] - 1 + 127, 0) - down, 1)
    scale = np.exp2(byte - 127.0)
    codes = (blocks / scale).astype(np.float32).astype(dtype).astype(np.float64)
    return np.moveaxis((codes * scale).reshape(v.shape), -1, axis)


WIDE = False


def mx_kscale(k):
    if not WIDE:
        return np.ones(k)
    levels = np.array([10, -10, 5, -5, 0])
    a = np.random.permutation(np.resize(levels, k // 512 * 4)).reshape(k // 512, 4)
    idx = np.arange(k)
    return np.exp2(a[idx // 512, idx % 128 // 32])


BF16 = ml_dtypes.bfloat16


def bf(x):
    return np.asarray(x, np.float32).astype(BF16)


def f64(x):
    return np.asarray(x).astype(np.float64)


E2M1 = np.array([0.0, 0.5, 1.0, 1.5, 2.0, 3.0, 4.0, 6.0, -0.0, -0.5, -1.0, -1.5, -2.0, -3.0, -4.0, -6.0])


def pack_weight(w, fmt):
    k, n = w.shape
    w = f64(bf(w)).reshape(k // 32, 32, n)
    amax = np.abs(w).max(1)
    if fmt == "e4m3":
        byte = np.frexp(amax)[1] - 1 + 127 - 7
    else:
        mant, ex = np.frexp(amax / 6.0)
        byte = np.where(mant > 0.5, ex, ex - 1) + 127
    byte = np.clip(np.where(amax > 0, byte, 1), 1, 254)
    scaled = (w * np.exp2(127.0 - byte)[:, None, :]).reshape(k, n).astype(np.float32)
    by_word = np.ascontiguousarray(scaled.reshape(k // 512, 128, 4, n).transpose(0, 1, 3, 2))
    if fmt == "e4m3":
        words = by_word.astype(ml_dtypes.float8_e4m3fn).view(np.uint8)
    else:
        c = by_word.astype(ml_dtypes.float4_e2m1fn).view(np.uint8) & 0xF
        words = c[..., 0::2] | (c[..., 1::2] << 4)
    return np.ascontiguousarray(words), np.ascontiguousarray(byte.astype(np.uint8).reshape(k // 512, 16, n))


def unpack_weight(words, scales, fmt):
    g, p, n, _ = words.shape
    if fmt == "e4m3":
        vals = np.ascontiguousarray(words).view(ml_dtypes.float8_e4m3fn).astype(np.float64)
    else:
        nib = np.empty((g, p, n, 4), np.uint8)
        nib[..., 0::2] = words & 0xF
        nib[..., 1::2] = words >> 4
        vals = E2M1[nib]
    vals = vals * np.repeat(np.exp2(scales.astype(np.float64) - 127.0), 8, axis=1)[..., None]
    return vals.transpose(0, 1, 3, 2).reshape(g * 512, n)


M, B, S, D = 3, 1, 512, 1024
F = D + D


def setup_inputs():
    s = mx_kscale(F)
    q = bf(np.random.standard_normal((M, B, S, D)) * 1.5)
    k = bf(np.random.standard_normal((M, B, S, D)) * 1.5)
    v = bf(np.random.standard_normal((M, B, S, D)) * s[D:])
    x = bf(np.random.standard_normal((M, B, S, D)) * s[:D])
    Wo = np.random.standard_normal((M, F, D)) / np.sqrt(D) / s[:, None]
    Wo_words, Wo_scales = pack_weight(Wo.reshape(-1, D), "e4m3")
    bo = bf(np.random.standard_normal((M, D)) * 0.3)
    return {
        "q": q,
        "k": k,
        "v": v,
        "x": x,
        "Wo_words": Wo_words,
        "Wo_scales": Wo_scales,
        "bo": bo,
    }


def reference(q, k, v, x, Wo_words, Wo_scales, bo):
    sc = (f64(q) @ f64(k).transpose(0, 1, 3, 2)) * (1.0 / np.sqrt(D))
    e = np.exp(sc - sc.max(-1, keepdims=True))
    v_next = np.roll(f64(v), -1, axis=0)
    ctx = (mxq(e, 3, "e4m3") @ mxq(v_next, 2, "e4m3")) / e.sum(-1, keepdims=True)
    comb = np.concatenate([f64(x), ctx], axis=-1)
    return (mxq(comb, 3, "e4m3") @ unpack_weight(Wo_words, Wo_scales, "e4m3").reshape(M, F, D)[:, None]) + f64(bo)[:, None, None, :]

@@ -1,0 +1,312 @@
+from contextlib import ExitStack
+
+import concourse.mybir as mybir
+from concourse.masks import make_identity
+
+BF16 = mybir.dt.bfloat16
+F32 = mybir.dt.float32
+I32 = mybir.dt.int32
+U32 = mybir.dt.uint32
+U8 = mybir.dt.uint8
+FP8X4 = mybir.dt.float8_e4m3fn_x4
+ACT = mybir.ActivationFunctionType
+ALU = mybir.AluOpType
+AXIS = mybir.AxisListType
+
+P = 128
+PACK = 4
+MODS = 3
+S = 512
+D = 1024
+TILES = S // P
+UNITS = MODS * TILES
+CHUNKS = D // P
+HALF = 512
+X_PASSES = D // (P * PACK)
+PASSES = 2 * X_PASSES
+SCALE = 1.0 / 32.0
+
+FLOPS = 2 * MODS * (S * S * D + S * S * D + S * 2 * D * D)
+
+
+def tile_trimodalcrossattention_ver2_pa_e_kernel(tc, q, k, v, x, Wo_words, Wo_scales, bo, out):
+    nc = tc.nc
+    with ExitStack() as stack:
+        const = stack.enter_context(tc.tile_pool(name="const", bufs=1))
+        loads = stack.enter_context(tc.tile_pool(name="loads", bufs=2))
+        work = stack.enter_context(tc.tile_pool(name="work", bufs=2))
+        psum_tp = stack.enter_context(tc.psum_pool(name="psum_tp", bufs=3))
+        psum_sc = stack.enter_context(tc.psum_pool(name="psum_sc", bufs=1))
+        psum_mid = stack.enter_context(tc.psum_pool(name="psum_mid", bufs=2))
+        psum_out = stack.enter_context(tc.psum_pool(name="psum_out", bufs=2))
+
+        ident_bf = const.tile([P, P], BF16, name="ident_bf")
+        make_identity(nc, ident_bf[:])
+        ident_f32 = const.tile([P, P], F32, name="ident_f32")
+        make_identity(nc, ident_f32[:])
+
+        wo_planes = const.tile([P, MODS, D], U8, name="wo_planes", align_bytes=64)
+        nc.vector.memset(wo_planes[:].rearrange("p m n -> p (m n)").bitcast(I32), 0)
+
+        q_raw, k_raw, v_raw, x_raw, wo_words, bias = {}, {}, {}, {}, {}, {}
+        kT, v_codes, v_plane = {}, {}, {}
+        qT, neg_max, e_rows, row_sum, recip_sq, recip_bc = {}, {}, {}, {}, {}, {}
+        e_codes, e_plane, comb_codes, comb_plane, ctx_psum = {}, {}, {}, {}, {}
+
+        def rows_on_partitions(dram_rows):
+            return dram_rows.rearrange("(p i) n -> p i n", i=TILES)
+
+        def load_tile_by_tile(table, m, dram, name):
+            table[m] = loads.tile([P, TILES, D], BF16, name=name, tag=name)
+            for i in range(TILES):
+                nc.sync.dma_start(out=table[m][:, i, :], in_=rows_on_partitions(dram[m, 0])[:, i, :])
+
+        def load_whole(table, m, dram_rows, name):
+            table[m] = loads.tile([P, TILES, D], BF16, name=name, tag=name)
+            nc.sync.dma_start(out=table[m][:], in_=rows_on_partitions(dram_rows))
+
+        def load_modality(m):
+            load_whole(v_raw, m, v[(m + 1) % MODS, 0], "v_raw")
+            if m + 1 < MODS:
+                load_tile_by_tile(k_raw, m + 1, k, "k_raw")
+            load_whole(x_raw, m, x[m, 0], "x_raw")
+            for quadrant in range(4):
+                nc.sync.dma_start(
+                    out=wo_planes[32 * quadrant : 32 * quadrant + 16, m, :].bitcast(I32),
+                    in_=Wo_scales[PASSES * m : PASSES * (m + 1), 4 * quadrant : 4 * quadrant + 4, :].bitcast(I32),
+                )
+            bias[m] = const.tile([P, D], BF16, name="bias%d" % m)
+            nc.sync.dma_start(out=bias[m][:], in_=bo[m].partition_broadcast(P))
+            wo_words[m] = const.tile([P, PASSES, D], I32, name="wo_words%d" % m, align_bytes=64)
+            for g in range(PASSES):
+                nc.sync.dma_start(
+                    out=wo_words[m][:, g, :],
+                    in_=Wo_words[PASSES * m + g].rearrange("p n t -> p (n t)").bitcast(I32),
+                )
+            if m + 1 < MODS:
+                load_tile_by_tile(q_raw, m + 1, q, "q_raw")
+
+        def scores_and_transposes(a):
+            next_q, key_tile, prev = a + 1, a + TILES, a - 1
+            if 0 <= a < UNITS:
+                scores = psum_sc.tile([P, S], F32, name="scores")
+            if 0 <= next_q < UNITS:
+                q_psum = psum_tp.tile([P, CHUNKS, P], BF16, name="q_psum", tag="tp")
+            if 0 <= key_tile < UNITS:
+                k_psum = psum_tp.tile([P, CHUNKS, P], BF16, name="k_psum", tag="tp")
+            if 0 <= prev < UNITS:
+                er_psum = psum_tp.tile([P, 3 * P], F32, name="er_psum", tag="tp")
+                eT_psum = er_psum[:, 0 : 2 * P].bitcast(BF16).rearrange("p (t r) -> p t r", t=PACK)
+            for c in range(CHUNKS):
+                if 0 <= a < UNITS:
+                    nc.tensor.matmul(
+                        out=scores[:],
+                        lhsT=qT[a][:, c, :],
+                        rhs=kT[a // TILES][:, c, :],
+                        start=(c == 0),
+                        stop=(c == CHUNKS - 1),
+                    )
+                first_half = c < CHUNKS // 2
+                pair = 2 * (c % (CHUNKS // 2))
+                for chunk in (pair, pair + 1):
+                    cols = slice(P * chunk, P * (chunk + 1))
+                    if first_half and 0 <= next_q < UNITS:
+                        source = q_raw[next_q // TILES][:, next_q % TILES, cols]
+                        nc.tensor.transpose(q_psum[:, chunk, :], source, ident_bf[:])
+                    if not first_half and 0 <= key_tile < UNITS:
+                        source = k_raw[key_tile // TILES][:, key_tile % TILES, cols]
+                        nc.tensor.transpose(k_psum[:, chunk, :], source, ident_bf[:])
+                if not first_half and 0 <= prev < UNITS:
+                    t = c - CHUNKS // 2
+                    nc.tensor.transpose(eT_psum[:, t, :], e_rows[prev][:, P * t : P * (t + 1)], ident_bf[:])
+            if 0 <= prev < UNITS:
+                nc.tensor.transpose(er_psum[:, 2 * P : 3 * P], recip_sq[prev][:], ident_f32[:])
+
+            if 0 <= next_q < UNITS:
+                qT[next_q] = work.tile([P, CHUNKS, P], BF16, name="qT", tag="qT")
+                nc.scalar.copy(out=qT[next_q][:], in_=q_psum[:])
+            if 0 <= a < UNITS:
+                softmax_maximum(a, scores)
+            if 0 <= prev < UNITS:
+                e_grouped = work.tile([P, P, PACK], BF16, name="e_grouped", tag="e_grouped", align_bytes=64)
+                nc.scalar.copy(out=e_grouped[:], in_=eT_psum.rearrange("p t r -> p r t"))
+                recip_bc[prev] = work.tile([P, P], F32, name="recip_bc", tag="recip_bc")
+                nc.scalar.copy(out=recip_bc[prev][:], in_=er_psum[:, 2 * P : 3 * P])
+            if 0 <= a < UNITS:
+                softmax_exponential(a, scores)
+            if 0 <= prev < UNITS:
+                e_codes[prev] = work.tile([P, P], U32, name="e_codes", tag="e_codes", align_bytes=64)
+                e_plane[prev] = work.tile([P, P], U8, name="e_plane", tag="e_plane", align_bytes=64)
+                nc.vector.quantize_mx(
+                    out=e_codes[prev][:].bitcast(FP8X4),
+                    scales=e_plane[prev][:],
+                    in_=e_grouped[:].rearrange("p r t -> p (r t)"),
+                )
+            if 0 <= key_tile < UNITS:
+                return k_psum
+            return None
+
+        def keys_leave_psum(key_tile, k_psum):
+            m, i = key_tile // TILES, key_tile % TILES
+            if i == 0:
+                kT[m] = work.tile([P, CHUNKS, S], BF16, name="kT", tag="kT")
+            nc.scalar.copy(out=kT[m][:, :, P * i : P * (i + 1)], in_=k_psum[:])
+
+
+        def softmax_maximum(a, scores):
+            row_max = work.tile([P, 1], F32, name="row_max", tag="row_max")
+            nc.vector.tensor_reduce(out=row_max[:], in_=scores[:], axis=AXIS.X, op=ALU.max)
+            neg_max[a] = work.tile([P, 1], F32, name="neg_max", tag="neg_max")
+            nc.vector.tensor_scalar(out=neg_max[a][:], in0=row_max[:], scalar1=-SCALE, scalar2=None, op0=ALU.mult)
+
+        def softmax_exponential(a, scores):
+            e_rows[a] = work.tile([P, S], BF16, name="e_rows", tag="e_rows")
+            row_sum[a] = work.tile([P, 1], F32, name="row_sum", tag="row_sum")
+            nc.scalar.activation(
+                out=e_rows[a][:],
+                in_=scores[:],
+                func=ACT.Exp,
+                bias=neg_max[a][:],
+                scale=SCALE,
+                accum_out=row_sum[a][:],
+            )
+
+        def reciprocal_square(a):
+            recip = work.tile([P, 1], F32, name="recip", tag="recip")
+            nc.vector.reciprocal(out=recip[:], in_=row_sum[a][:])
+            recip_sq[a] = work.tile([P, P], F32, name="recip_sq", tag="recip_sq")
+            nc.vector.tensor_copy(out=recip_sq[a][:], in_=recip[:].to_broadcast([P, P]))
+
+        def regroup_values(m, g):
+            grouped = work.tile([P, PACK * P * PACK], BF16, name="v_grouped", tag="v_grouped", align_bytes=64)
+            nc.vector.tensor_copy(
+                out=grouped[:].rearrange("p (t r j) -> p r j t", t=PACK, j=PACK),
+                in_=v_raw[m][:, :, HALF * g : HALF * (g + 1)].rearrange("p j (r t) -> p r j t", t=PACK),
+            )
+            return grouped
+
+        def quantise_values(m, g, grouped):
+            if g == 0:
+                v_codes[m] = work.tile([P, D], U32, name="v_codes", tag="v_codes", align_bytes=64)
+                v_plane[m] = work.tile([P, D], U8, name="v_plane", tag="v_plane", align_bytes=64)
+            cols = slice(HALF * g, HALF * (g + 1))
+            nc.vector.quantize_mx(out=v_codes[m][:, cols].bitcast(FP8X4), scales=v_plane[m][:, cols], in_=grouped[:])
+
+        def transpose_x(u):
+            words = x_raw[u // TILES][:, u % TILES, :].bitcast(F32)
+            x_psum = psum_mid.tile([P, X_PASSES, 2, P], F32, name="x_psum", tag="mid")
+            for g in range(X_PASSES):
+                for w in range(2):
+                    nc.tensor.transpose(x_psum[:, g, w, :], words[:, 256 * g + w : 256 * (g + 1) : 2], ident_f32[:])
+            return x_psum
+
+        def x_leaves_psum(x_psum):
+            x_grouped = work.tile([P, X_PASSES * P * PACK], BF16, name="x_grouped", tag="x_grouped", align_bytes=64)
+            nc.scalar.copy(
+                out=x_grouped[:].bitcast(F32).rearrange("p (g r w) -> p g r w", g=X_PASSES, w=2),
+                in_=x_psum[:].rearrange("p g w r -> p g r w"),
+            )
+            return x_grouped
+
+        def quantise_x(u, x_grouped):
+            comb_codes[u] = work.tile([P, PASSES * P], U32, name="comb_codes", tag="comb_codes", bufs=3, align_bytes=64)
+            comb_plane[u] = work.tile([P, PASSES * P], U8, name="comb_plane", tag="comb_plane", bufs=3, align_bytes=64)
+            cols = slice(0, X_PASSES * P)
+            nc.vector.quantize_mx(
+                out=comb_codes[u][:, cols].bitcast(FP8X4), scales=comb_plane[u][:, cols], in_=x_grouped[:]
+            )
+
+        def context_products(u):
+            m = u // TILES
+            ctx_psum[u] = []
+            for g in range(X_PASSES):
+                bank = psum_mid.tile([P, PACK, P], F32, name="ctx_psum", tag="mid")
+                for t in range(PACK):
+                    cols = slice(P * (PACK * g + t), P * (PACK * g + t + 1))
+                    nc.tensor.matmul_mx(
+                        out=bank[:, t, :],
+                        lhsT=v_codes[m][:, cols].bitcast(FP8X4),
+                        lhsT_scale=v_plane[m][:, cols],
+                        rhs=e_codes[u][:].bitcast(FP8X4),
+                        rhs_scale=e_plane[u][:],
+                        start=True,
+                        stop=True,
+                    )
+                ctx_psum[u].append(bank)
+
+        def normalise_and_quantise_context(u):
+            grouped = []
+            for g in range(X_PASSES):
+                ctx_grouped = work.tile([P, P, PACK], BF16, name="ctx_grouped", tag="ctx_grouped", align_bytes=64)
+                nc.vector.tensor_tensor(
+                    out=ctx_grouped[:],
+                    in0=ctx_psum[u][g][:].rearrange("p t r -> p r t"),
+                    in1=recip_bc[u][:].unsqueeze(2).to_broadcast([P, P, PACK]),
+                    op=ALU.mult,
+                )
+                grouped.append(ctx_grouped)
+            for g in range(X_PASSES):
+                cols = slice(P * (X_PASSES + g), P * (X_PASSES + g + 1))
+                nc.vector.quantize_mx(
+                    out=comb_codes[u][:, cols].bitcast(FP8X4),
+                    scales=comb_plane[u][:, cols],
+                    in_=grouped[g][:].rearrange("p r t -> p (r t)"),
+                )
+
+        def output_products(u):
+            m = u // TILES
+            banks = []
+            for h in range(D // HALF):
+                banks.append(psum_out.tile([P, HALF], F32, name="out_psum", tag="out_psum"))
+            for g in range(PASSES):
+                for h in range(D // HALF):
+                    nc.tensor.matmul_mx(
+                        out=banks[h][:],
+                        lhsT=comb_codes[u][:, P * g : P * (g + 1)].bitcast(FP8X4),
+                        lhsT_scale=comb_plane[u][:, P * g : P * (g + 1)],
+                        rhs=wo_words[m][:, g, HALF * h : HALF * (h + 1)].bitcast(FP8X4),
+                        rhs_scale=wo_planes[4 * g : P, m, HALF * h : HALF * (h + 1)],
+                        start=(g == 0),
+                        stop=(g == PASSES - 1),
+                    )
+            return banks
+
+        def add_bias_and_store(u, banks):
+            m, i = u // TILES, u % TILES
+            for h in range(D // HALF):
+                cols = slice(HALF * h, HALF * (h + 1))
+                result = work.tile([P, HALF], F32, name="result", tag="result", bufs=4)
+                nc.vector.tensor_tensor(out=result[:], in0=banks[h][:], in1=bias[m][:, cols], op=ALU.add)
+                nc.gpsimd.dma_start(out=rows_on_partitions(out[m, 0])[:, i, cols], in_=result[:])
+
+        with tc.manual_schedule():
+            load_tile_by_tile(k_raw, 0, k, "k_raw")
+            load_tile_by_tile(q_raw, 0, q, "q_raw")
+            for step in range(-TILES, UNITS + 2):
+                a, b, c = step, step - 1, step - 2
+                ahead = step + 1
+                if ahead % TILES == 0 and ahead < UNITS:
+                    load_modality(ahead // TILES)
+                if 0 <= c < UNITS:
+                    normalise_and_quantise_context(c)
+                k_psum = scores_and_transposes(a)
+                values_half = ahead % TILES
+                if values_half < X_PASSES and 0 <= ahead - values_half < UNITS:
+                    v_grouped = regroup_values(ahead // TILES, values_half)
+                if 0 <= b < UNITS:
+                    x_psum = transpose_x(b)
+                    x_grouped = x_leaves_psum(x_psum)
+                if k_psum is not None:
+                    keys_leave_psum(a + TILES, k_psum)
+                if 0 <= b < UNITS:
+                    quantise_x(b, x_grouped)
+                if 0 <= a < UNITS:
+                    reciprocal_square(a)
+                if values_half < X_PASSES and 0 <= ahead - values_half < UNITS:
+                    quantise_values(ahead // TILES, values_half, v_grouped)
+                if 0 <= c < UNITS:
+                    out_banks = output_products(c)
+                if 0 <= b < UNITS:
+                    context_products(b)
+                if 0 <= c < UNITS:
+                    add_bias_and_store(c, out_banks)

@@ -20,7 +20,7 @@ S = 512
 D = 1024
 TILES = S // P
 UNITS = MODS * TILES
-CHUNKS = D // P
+WORD_CHUNKS = D // (2 * P)
 HALF = 512
 X_PASSES = D // (P * PACK)
 PASSES = 2 * X_PASSES
@@ -37,11 +37,9 @@ def tile_trimodalcrossattention_ver2_pa_e_kernel(tc, q, k, v, x, Wo_words, Wo_sc
         work = stack.enter_context(tc.tile_pool(name="work", bufs=2))
         psum_tp = stack.enter_context(tc.psum_pool(name="psum_tp", bufs=3))
         psum_sc = stack.enter_context(tc.psum_pool(name="psum_sc", bufs=1))
-        psum_mid = stack.enter_context(tc.psum_pool(name="psum_mid", bufs=2))
+        psum_ctx = stack.enter_context(tc.psum_pool(name="psum_ctx", bufs=2))
         psum_out = stack.enter_context(tc.psum_pool(name="psum_out", bufs=2))
 
-        ident_bf = const.tile([P, P], BF16, name="ident_bf")
-        make_identity(nc, ident_bf[:])
         ident_f32 = const.tile([P, P], F32, name="ident_f32")
         make_identity(nc, ident_f32[:])
 
@@ -51,7 +49,7 @@ def tile_trimodalcrossattention_ver2_pa_e_kernel(tc, q, k, v, x, Wo_words, Wo_sc
         q_raw, k_raw, v_raw, x_raw, wo_words, bias = {}, {}, {}, {}, {}, {}
         kT, v_codes, v_plane = {}, {}, {}
         qT, neg_max, e_rows, row_sum, recip_sq, recip_bc = {}, {}, {}, {}, {}, {}
-        e_codes, e_plane, comb_codes, comb_plane, ctx_psum = {}, {}, {}, {}, {}
+        e_codes, e_plane, comb_codes, comb_plane, ctx_psum, x_sorted = {}, {}, {}, {}, {}, {}
 
         def rows_on_partitions(dram_rows):
             return dram_rows.rearrange("(p i) n -> p i n", i=TILES)
@@ -66,9 +64,9 @@ def tile_trimodalcrossattention_ver2_pa_e_kernel(tc, q, k, v, x, Wo_words, Wo_sc
             nc.sync.dma_start(out=table[m][:], in_=rows_on_partitions(dram_rows))
 
         def load_modality(m):
-            load_whole(v_raw, m, v[(m + 1) % MODS, 0], "v_raw")
             if m + 1 < MODS:
                 load_tile_by_tile(k_raw, m + 1, k, "k_raw")
+            load_whole(v_raw, m, v[(m + 1) % MODS, 0], "v_raw")
             load_whole(x_raw, m, x[m, 0], "x_raw")
             for quadrant in range(4):
                 nc.sync.dma_start(
@@ -90,48 +88,51 @@ def tile_trimodalcrossattention_ver2_pa_e_kernel(tc, q, k, v, x, Wo_words, Wo_sc
             next_q, key_tile, prev = a + 1, a + TILES, a - 1
             if 0 <= a < UNITS:
                 scores = psum_sc.tile([P, S], F32, name="scores")
+                q_pairs = qT[a][:].rearrange("p c (r e) -> p c r e", e=2)
+                k_pairs = kT[a // TILES][:].rearrange("p c (r e) -> p c r e", e=2)
             if 0 <= next_q < UNITS:
-                q_psum = psum_tp.tile([P, CHUNKS, P], BF16, name="q_psum", tag="tp")
+                q_psum = psum_tp.tile([P, WORD_CHUNKS, P], F32, name="q_psum", tag="tp")
+                q_words = q_raw[next_q // TILES][:, next_q % TILES, :].bitcast(F32)
             if 0 <= key_tile < UNITS:
-                k_psum = psum_tp.tile([P, CHUNKS, P], BF16, name="k_psum", tag="tp")
+                k_psum = psum_tp.tile([P, WORD_CHUNKS, P], F32, name="k_psum", tag="tp")
+                k_words = k_raw[key_tile // TILES][:, key_tile % TILES, :].bitcast(F32)
             if 0 <= prev < UNITS:
-                er_psum = psum_tp.tile([P, 3 * P], F32, name="er_psum", tag="tp")
-                eT_psum = er_psum[:, 0 : 2 * P].bitcast(BF16).rearrange("p (t r) -> p t r", t=PACK)
-            for c in range(CHUNKS):
-                if 0 <= a < UNITS:
-                    nc.tensor.matmul(
-                        out=scores[:],
-                        lhsT=qT[a][:, c, :],
-                        rhs=kT[a // TILES][:, c, :],
-                        start=(c == 0),
-                        stop=(c == CHUNKS - 1),
-                    )
-                first_half = c < CHUNKS // 2
-                pair = 2 * (c % (CHUNKS // 2))
-                for chunk in (pair, pair + 1):
-                    cols = slice(P * chunk, P * (chunk + 1))
-                    if first_half and 0 <= next_q < UNITS:
-                        source = q_raw[next_q // TILES][:, next_q % TILES, cols]
-                        nc.tensor.transpose(q_psum[:, chunk, :], source, ident_bf[:])
-                    if not first_half and 0 <= key_tile < UNITS:
-                        source = k_raw[key_tile // TILES][:, key_tile % TILES, cols]
-                        nc.tensor.transpose(k_psum[:, chunk, :], source, ident_bf[:])
-                if not first_half and 0 <= prev < UNITS:
-                    t = c - CHUNKS // 2
-                    nc.tensor.transpose(eT_psum[:, t, :], e_rows[prev][:, P * t : P * (t + 1)], ident_bf[:])
+                er_psum = psum_tp.tile([P, 3, P], F32, name="er_psum", tag="tp")
+                e_words = e_rows[prev][:].bitcast(F32)
+            for c in range(WORD_CHUNKS):
+                for e in range(2):
+                    if 0 <= a < UNITS:
+                        nc.tensor.matmul(
+                            out=scores[:],
+                            lhsT=q_pairs[:, c, :, e],
+                            rhs=k_pairs[:, c, :, e],
+                            start=(c == 0 and e == 0),
+                            stop=(c == WORD_CHUNKS - 1 and e == 1),
+                        )
+                    turn = 2 * c + e
+                    if turn < WORD_CHUNKS and 0 <= next_q < UNITS:
+                        nc.tensor.transpose(q_psum[:, turn, :], q_words[:, P * turn : P * (turn + 1)], ident_f32[:])
+                    if turn >= WORD_CHUNKS and 0 <= key_tile < UNITS:
+                        t = turn - WORD_CHUNKS
+                        nc.tensor.transpose(k_psum[:, t, :], k_words[:, P * t : P * (t + 1)], ident_f32[:])
             if 0 <= prev < UNITS:
-                nc.tensor.transpose(er_psum[:, 2 * P : 3 * P], recip_sq[prev][:], ident_f32[:])
+                for w in range(2):
+                    nc.tensor.transpose(er_psum[:, w, :], e_words[:, P * w : P * (w + 1)], ident_f32[:])
+                nc.tensor.transpose(er_psum[:, 2, :], recip_sq[prev][:], ident_f32[:])
 
             if 0 <= next_q < UNITS:
-                qT[next_q] = work.tile([P, CHUNKS, P], BF16, name="qT", tag="qT")
-                nc.scalar.copy(out=qT[next_q][:], in_=q_psum[:])
+                qT[next_q] = work.tile([P, WORD_CHUNKS, 2 * P], BF16, name="qT", tag="qT")
+                nc.scalar.copy(out=qT[next_q][:].bitcast(F32), in_=q_psum[:])
             if 0 <= a < UNITS:
                 softmax_maximum(a, scores)
             if 0 <= prev < UNITS:
-                e_grouped = work.tile([P, P, PACK], BF16, name="e_grouped", tag="e_grouped", align_bytes=64)
-                nc.scalar.copy(out=e_grouped[:], in_=eT_psum.rearrange("p t r -> p r t"))
+                e_grouped = work.tile([P, P * PACK], BF16, name="e_grouped", tag="e_grouped", align_bytes=64)
+                nc.scalar.copy(
+                    out=e_grouped[:].bitcast(F32).rearrange("p (r w) -> p r w", w=2),
+                    in_=er_psum[:, 0:2, :].rearrange("p w r -> p r w"),
+                )
                 recip_bc[prev] = work.tile([P, P], F32, name="recip_bc", tag="recip_bc")
-                nc.scalar.copy(out=recip_bc[prev][:], in_=er_psum[:, 2 * P : 3 * P])
+                nc.scalar.copy(out=recip_bc[prev][:], in_=er_psum[:, 2, :])
             if 0 <= a < UNITS:
                 softmax_exponential(a, scores)
             if 0 <= prev < UNITS:
@@ -140,7 +141,7 @@ def tile_trimodalcrossattention_ver2_pa_e_kernel(tc, q, k, v, x, Wo_words, Wo_sc
                 nc.vector.quantize_mx(
                     out=e_codes[prev][:].bitcast(FP8X4),
                     scales=e_plane[prev][:],
-                    in_=e_grouped[:].rearrange("p r t -> p (r t)"),
+                    in_=e_grouped[:],
                 )
             if 0 <= key_tile < UNITS:
                 return k_psum
@@ -149,8 +150,8 @@ def tile_trimodalcrossattention_ver2_pa_e_kernel(tc, q, k, v, x, Wo_words, Wo_sc
         def keys_leave_psum(key_tile, k_psum):
             m, i = key_tile // TILES, key_tile % TILES
             if i == 0:
-                kT[m] = work.tile([P, CHUNKS, S], BF16, name="kT", tag="kT")
-            nc.scalar.copy(out=kT[m][:, :, P * i : P * (i + 1)], in_=k_psum[:])
+                kT[m] = work.tile([P, WORD_CHUNKS, 2 * S], BF16, name="kT", tag="kT")
+            nc.scalar.copy(out=kT[m][:].bitcast(F32)[:, :, P * i : P * (i + 1)], in_=k_psum[:])
 
 
         def softmax_maximum(a, scores):
@@ -163,8 +164,8 @@ def tile_trimodalcrossattention_ver2_pa_e_kernel(tc, q, k, v, x, Wo_words, Wo_sc
             e_rows[a] = work.tile([P, S], BF16, name="e_rows", tag="e_rows")
             row_sum[a] = work.tile([P, 1], F32, name="row_sum", tag="row_sum")
             nc.scalar.activation(
-                out=e_rows[a][:],
-                in_=scores[:],
+                out=e_rows[a][:].rearrange("r (w p e) -> r w p e", w=2, e=2),
+                in_=scores[:].rearrange("r (w e p) -> r w p e", w=2, e=2),
                 func=ACT.Exp,
                 bias=neg_max[a][:],
                 scale=SCALE,
@@ -192,12 +193,16 @@ def tile_trimodalcrossattention_ver2_pa_e_kernel(tc, q, k, v, x, Wo_words, Wo_sc
             cols = slice(HALF * g, HALF * (g + 1))
             nc.vector.quantize_mx(out=v_codes[m][:, cols].bitcast(FP8X4), scales=v_plane[m][:, cols], in_=grouped[:])
 
-        def transpose_x(u):
+        def sort_x(u):
             words = x_raw[u // TILES][:, u % TILES, :].bitcast(F32)
-            x_psum = psum_mid.tile([P, X_PASSES, 2, P], F32, name="x_psum", tag="mid")
+            x_sorted[u] = work.tile([P, X_PASSES, 2, P], F32, name="x_sorted", tag="x_sorted")
+            nc.scalar.copy(out=x_sorted[u][:], in_=words.rearrange("r (g p w) -> r g w p", g=X_PASSES, w=2))
+
+        def transpose_x(u):
+            x_psum = psum_tp.tile([P, X_PASSES, 2, P], F32, name="x_psum", tag="tp")
             for g in range(X_PASSES):
                 for w in range(2):
-                    nc.tensor.transpose(x_psum[:, g, w, :], words[:, 256 * g + w : 256 * (g + 1) : 2], ident_f32[:])
+                    nc.tensor.transpose(x_psum[:, g, w, :], x_sorted[u][:, g, w, :], ident_f32[:])
             return x_psum
 
         def x_leaves_psum(x_psum):
@@ -220,7 +225,7 @@ def tile_trimodalcrossattention_ver2_pa_e_kernel(tc, q, k, v, x, Wo_words, Wo_sc
             m = u // TILES
             ctx_psum[u] = []
             for g in range(X_PASSES):
-                bank = psum_mid.tile([P, PACK, P], F32, name="ctx_psum", tag="mid")
+                bank = psum_ctx.tile([P, PACK, P], F32, name="ctx_psum", tag="ctx_psum")
                 for t in range(PACK):
                     cols = slice(P * (PACK * g + t), P * (PACK * g + t + 1))
                     nc.tensor.matmul_mx(
@@ -282,31 +287,30 @@ def tile_trimodalcrossattention_ver2_pa_e_kernel(tc, q, k, v, x, Wo_words, Wo_sc
         with tc.manual_schedule():
             load_tile_by_tile(k_raw, 0, k, "k_raw")
             load_tile_by_tile(q_raw, 0, q, "q_raw")
-            for step in range(-TILES, UNITS + 2):
-                a, b, c = step, step - 1, step - 2
-                ahead = step + 1
-                if ahead % TILES == 0 and ahead < UNITS:
-                    load_modality(ahead // TILES)
-                if 0 <= c < UNITS:
-                    normalise_and_quantise_context(c)
-                k_psum = scores_and_transposes(a)
-                values_half = ahead % TILES
-                if values_half < X_PASSES and 0 <= ahead - values_half < UNITS:
-                    v_grouped = regroup_values(ahead // TILES, values_half)
-                if 0 <= b < UNITS:
-                    x_psum = transpose_x(b)
+            for step in range(-TILES, UNITS + 3):
+                u_scores, u_ctx, u_out = step, step - 2, step - 3
+                if (step + 1) % TILES == 0 and step + 1 < UNITS:
+                    load_modality((step + 1) // TILES)
+                if 0 <= u_ctx < UNITS:
+                    sort_x(u_ctx)
+                k_psum = scores_and_transposes(u_scores)
+                values_due = 0 <= u_scores < UNITS and u_scores % TILES < X_PASSES
+                if values_due:
+                    v_grouped = regroup_values(u_scores // TILES, u_scores % TILES)
+                if 0 <= u_ctx < UNITS:
+                    x_psum = transpose_x(u_ctx)
                     x_grouped = x_leaves_psum(x_psum)
                 if k_psum is not None:
-                    keys_leave_psum(a + TILES, k_psum)
-                if 0 <= b < UNITS:
-                    quantise_x(b, x_grouped)
-                if 0 <= a < UNITS:
-                    reciprocal_square(a)
-                if values_half < X_PASSES and 0 <= ahead - values_half < UNITS:
-                    quantise_values(ahead // TILES, values_half, v_grouped)
-                if 0 <= c < UNITS:
-                    out_banks = output_products(c)
-                if 0 <= b < UNITS:
-                    context_products(b)
-                if 0 <= c < UNITS:
-                    add_bias_and_store(c, out_banks)
+                    keys_leave_psum(u_scores + TILES, k_psum)
+                if 0 <= u_ctx < UNITS:
+                    quantise_x(u_ctx, x_grouped)
+                if 0 <= u_scores < UNITS:
+                    reciprocal_square(u_scores)
+                if values_due:
+                    quantise_values(u_scores // TILES, u_scores % TILES, v_grouped)
+                if 0 <= u_ctx < UNITS:
+                    context_products(u_ctx)
+                    normalise_and_quantise_context(u_ctx)
+                if 0 <= u_out < UNITS:
+                    out_banks = output_products(u_out)
+                    add_bias_and_store(u_out, out_banks)

@@ -35,10 +35,7 @@ def tile_trimodalcrossattention_ver2_pa_e_kernel(tc, q, k, v, x, Wo_words, Wo_sc
         const = stack.enter_context(tc.tile_pool(name="const", bufs=1))
         loads = stack.enter_context(tc.tile_pool(name="loads", bufs=2))
         work = stack.enter_context(tc.tile_pool(name="work", bufs=2))
-        psum_tp = stack.enter_context(tc.psum_pool(name="psum_tp", bufs=3))
-        psum_sc = stack.enter_context(tc.psum_pool(name="psum_sc", bufs=1))
-        psum_ctx = stack.enter_context(tc.psum_pool(name="psum_ctx", bufs=2))
-        psum_out = stack.enter_context(tc.psum_pool(name="psum_out", bufs=2))
+        psum = stack.enter_context(tc.psum_pool(name="psum", bufs=8))
 
         ident_f32 = const.tile([P, P], F32, name="ident_f32")
         make_identity(nc, ident_f32[:])
@@ -87,17 +84,17 @@ def tile_trimodalcrossattention_ver2_pa_e_kernel(tc, q, k, v, x, Wo_words, Wo_sc
         def scores_and_transposes(a):
             next_q, key_tile, prev = a + 1, a + TILES, a - 1
             if 0 <= a < UNITS:
-                scores = psum_sc.tile([P, S], F32, name="scores")
+                scores = psum.tile([P, S], F32, name="scores", tag="bank")
                 q_pairs = qT[a][:].rearrange("p c (r e) -> p c r e", e=2)
                 k_pairs = kT[a // TILES][:].rearrange("p c (r e) -> p c r e", e=2)
             if 0 <= next_q < UNITS:
-                q_psum = psum_tp.tile([P, WORD_CHUNKS, P], F32, name="q_psum", tag="tp")
+                q_psum = psum.tile([P, WORD_CHUNKS, P], F32, name="q_psum", tag="bank")
                 q_words = q_raw[next_q // TILES][:, next_q % TILES, :].bitcast(F32)
             if 0 <= key_tile < UNITS:
-                k_psum = psum_tp.tile([P, WORD_CHUNKS, P], F32, name="k_psum", tag="tp")
+                k_psum = psum.tile([P, WORD_CHUNKS, P], F32, name="k_psum", tag="bank")
                 k_words = k_raw[key_tile // TILES][:, key_tile % TILES, :].bitcast(F32)
             if 0 <= prev < UNITS:
-                er_psum = psum_tp.tile([P, 3, P], F32, name="er_psum", tag="tp")
+                er_psum = psum.tile([P, 3, P], F32, name="er_psum", tag="bank")
                 e_words = e_rows[prev][:].bitcast(F32)
             for c in range(WORD_CHUNKS):
                 for e in range(2):
@@ -199,7 +196,7 @@ def tile_trimodalcrossattention_ver2_pa_e_kernel(tc, q, k, v, x, Wo_words, Wo_sc
             nc.scalar.copy(out=x_sorted[u][:], in_=words.rearrange("r (g p w) -> r g w p", g=X_PASSES, w=2))
 
         def transpose_x(u):
-            x_psum = psum_tp.tile([P, X_PASSES, 2, P], F32, name="x_psum", tag="tp")
+            x_psum = psum.tile([P, X_PASSES, 2, P], F32, name="x_psum", tag="bank")
             for g in range(X_PASSES):
                 for w in range(2):
                     nc.tensor.transpose(x_psum[:, g, w, :], x_sorted[u][:, g, w, :], ident_f32[:])
@@ -225,7 +222,7 @@ def tile_trimodalcrossattention_ver2_pa_e_kernel(tc, q, k, v, x, Wo_words, Wo_sc
             m = u // TILES
             ctx_psum[u] = []
             for g in range(X_PASSES):
-                bank = psum_ctx.tile([P, PACK, P], F32, name="ctx_psum", tag="ctx_psum")
+                bank = psum.tile([P, PACK, P], F32, name="ctx_psum", tag="bank")
                 for t in range(PACK):
                     cols = slice(P * (PACK * g + t), P * (PACK * g + t + 1))
                     nc.tensor.matmul_mx(
@@ -262,9 +259,8 @@ def tile_trimodalcrossattention_ver2_pa_e_kernel(tc, q, k, v, x, Wo_words, Wo_sc
             m = u // TILES
             banks = []
             for h in range(D // HALF):
-                banks.append(psum_out.tile([P, HALF], F32, name="out_psum", tag="out_psum"))
-            for g in range(PASSES):
-                for h in range(D // HALF):
+                banks.append(psum.tile([P, HALF], F32, name="out_psum", tag="bank"))
+                for g in range(PASSES):
                     nc.tensor.matmul_mx(
                         out=banks[h][:],
                         lhsT=comb_codes[u][:, P * g : P * (g + 1)].bitcast(FP8X4),
@@ -282,7 +278,7 @@ def tile_trimodalcrossattention_ver2_pa_e_kernel(tc, q, k, v, x, Wo_words, Wo_sc
                 cols = slice(HALF * h, HALF * (h + 1))
                 result = work.tile([P, HALF], F32, name="result", tag="result", bufs=4)
                 nc.vector.tensor_tensor(out=result[:], in0=banks[h][:], in1=bias[m][:, cols], op=ALU.add)
-                nc.gpsimd.dma_start(out=rows_on_partitions(out[m, 0])[:, i, cols], in_=result[:])
+                nc.sync.dma_start(out=rows_on_partitions(out[m, 0])[:, i, cols], in_=result[:])
 
         with tc.manual_schedule():
             load_tile_by_tile(k_raw, 0, k, "k_raw")

@@ -82,67 +82,64 @@ def tile_trimodalcrossattention_ver2_pa_e_kernel(tc, q, k, v, x, Wo_words, Wo_sc
                 load_tile_by_tile(q_raw, m + 1, q, "q_raw")
 
         def scores_and_transposes(a):
-            next_q, key_tile, prev = a + 1, a + TILES, a - 1
+            next_q, key_tile, u_e, u_x = a + 1, a + TILES, a - 2, a - 3
+            filled = {}
             if 0 <= a < UNITS:
-                scores = psum.tile([P, S], F32, name="scores", tag="bank")
+                filled["scores"] = psum.tile([P, S], F32, name="scores", tag="bank")
                 q_pairs = qT[a][:].rearrange("p c (r e) -> p c r e", e=2)
                 k_pairs = kT[a // TILES][:].rearrange("p c (r e) -> p c r e", e=2)
             if 0 <= next_q < UNITS:
-                q_psum = psum.tile([P, WORD_CHUNKS, P], F32, name="q_psum", tag="bank")
+                filled["q"] = psum.tile([P, WORD_CHUNKS, P], F32, name="q_psum", tag="bank")
                 q_words = q_raw[next_q // TILES][:, next_q % TILES, :].bitcast(F32)
+            if 0 <= u_x < UNITS:
+                filled["x"] = psum.tile([P, 2 * X_PASSES, P], F32, name="x_psum", tag="bank")
             if 0 <= key_tile < UNITS:
-                k_psum = psum.tile([P, WORD_CHUNKS, P], F32, name="k_psum", tag="bank")
+                filled["k"] = psum.tile([P, WORD_CHUNKS, P], F32, name="k_psum", tag="bank")
                 k_words = k_raw[key_tile // TILES][:, key_tile % TILES, :].bitcast(F32)
-            if 0 <= prev < UNITS:
-                er_psum = psum.tile([P, 3, P], F32, name="er_psum", tag="bank")
-                e_words = e_rows[prev][:].bitcast(F32)
+            if 0 <= u_e < UNITS:
+                filled["er"] = psum.tile([P, 3, P], F32, name="er_psum", tag="bank")
+                e_words = e_rows[u_e][:].bitcast(F32)
+                er_sources = [e_words[:, 0:P], e_words[:, P : 2 * P], recip_sq[u_e][:]]
             for c in range(WORD_CHUNKS):
                 for e in range(2):
                     if 0 <= a < UNITS:
                         nc.tensor.matmul(
-                            out=scores[:],
+                            out=filled["scores"][:],
                             lhsT=q_pairs[:, c, :, e],
                             rhs=k_pairs[:, c, :, e],
                             start=(c == 0 and e == 0),
                             stop=(c == WORD_CHUNKS - 1 and e == 1),
                         )
                     turn = 2 * c + e
-                    if turn < WORD_CHUNKS and 0 <= next_q < UNITS:
-                        nc.tensor.transpose(q_psum[:, turn, :], q_words[:, P * turn : P * (turn + 1)], ident_f32[:])
-                    if turn >= WORD_CHUNKS and 0 <= key_tile < UNITS:
-                        t = turn - WORD_CHUNKS
-                        nc.tensor.transpose(k_psum[:, t, :], k_words[:, P * t : P * (t + 1)], ident_f32[:])
-            if 0 <= prev < UNITS:
-                for w in range(2):
-                    nc.tensor.transpose(er_psum[:, w, :], e_words[:, P * w : P * (w + 1)], ident_f32[:])
-                nc.tensor.transpose(er_psum[:, 2, :], recip_sq[prev][:], ident_f32[:])
+                    late = turn - WORD_CHUNKS
+                    if late < 0 and 0 <= next_q < UNITS:
+                        nc.tensor.transpose(filled["q"][:, turn, :], q_words[:, P * turn : P * (turn + 1)], ident_f32[:])
+                    if late < 0 and 0 <= u_x < UNITS:
+                        nc.tensor.transpose(filled["x"][:, turn, :], x_sorted[u_x][:, turn, :], ident_f32[:])
+                    if late >= 0 and 0 <= key_tile < UNITS:
+                        nc.tensor.transpose(filled["k"][:, late, :], k_words[:, P * late : P * (late + 1)], ident_f32[:])
+                    if 0 <= late < 3 and 0 <= u_e < UNITS:
+                        nc.tensor.transpose(filled["er"][:, late, :], er_sources[late], ident_f32[:])
+            return filled
 
-            if 0 <= next_q < UNITS:
-                qT[next_q] = work.tile([P, WORD_CHUNKS, 2 * P], BF16, name="qT", tag="qT")
-                nc.scalar.copy(out=qT[next_q][:].bitcast(F32), in_=q_psum[:])
-            if 0 <= a < UNITS:
-                softmax_maximum(a, scores)
-            if 0 <= prev < UNITS:
-                e_grouped = work.tile([P, P * PACK], BF16, name="e_grouped", tag="e_grouped", align_bytes=64)
-                nc.scalar.copy(
-                    out=e_grouped[:].bitcast(F32).rearrange("p (r w) -> p r w", w=2),
-                    in_=er_psum[:, 0:2, :].rearrange("p w r -> p r w"),
-                )
-                recip_bc[prev] = work.tile([P, P], F32, name="recip_bc", tag="recip_bc")
-                nc.scalar.copy(out=recip_bc[prev][:], in_=er_psum[:, 2, :])
-            if 0 <= a < UNITS:
-                softmax_exponential(a, scores)
-            if 0 <= prev < UNITS:
-                e_codes[prev] = work.tile([P, P], U32, name="e_codes", tag="e_codes", align_bytes=64)
-                e_plane[prev] = work.tile([P, P], U8, name="e_plane", tag="e_plane", align_bytes=64)
-                nc.vector.quantize_mx(
-                    out=e_codes[prev][:].bitcast(FP8X4),
-                    scales=e_plane[prev][:],
-                    in_=e_grouped[:],
-                )
-            if 0 <= key_tile < UNITS:
-                return k_psum
-            return None
+        def queries_leave_psum(u, q_psum):
+            qT[u] = work.tile([P, WORD_CHUNKS, 2 * P], BF16, name="qT", tag="qT")
+            nc.scalar.copy(out=qT[u][:].bitcast(F32), in_=q_psum[:])
+
+        def e_and_reciprocal_leave_psum(u, er_psum):
+            e_grouped = work.tile([P, P * PACK], BF16, name="e_grouped", tag="e_grouped", align_bytes=64)
+            nc.scalar.copy(
+                out=e_grouped[:].bitcast(F32).rearrange("p (r w) -> p r w", w=2),
+                in_=er_psum[:, 0:2, :].rearrange("p w r -> p r w"),
+            )
+            recip_bc[u] = work.tile([P, P], F32, name="recip_bc", tag="recip_bc")
+            nc.scalar.copy(out=recip_bc[u][:], in_=er_psum[:, 2, :])
+            return e_grouped
+
+        def quantise_e(u, e_grouped):
+            e_codes[u] = work.tile([P, P], U32, name="e_codes", tag="e_codes", align_bytes=64)
+            e_plane[u] = work.tile([P, P], U8, name="e_plane", tag="e_plane", align_bytes=64)
+            nc.vector.quantize_mx(out=e_codes[u][:].bitcast(FP8X4), scales=e_plane[u][:], in_=e_grouped[:])
 
         def keys_leave_psum(key_tile, k_psum):
             m, i = key_tile // TILES, key_tile % TILES
@@ -158,7 +155,7 @@ def tile_trimodalcrossattention_ver2_pa_e_kernel(tc, q, k, v, x, Wo_words, Wo_sc
             nc.vector.tensor_scalar(out=neg_max[a][:], in0=row_max[:], scalar1=-SCALE, scalar2=None, op0=ALU.mult)
 
         def softmax_exponential(a, scores):
-            e_rows[a] = work.tile([P, S], BF16, name="e_rows", tag="e_rows")
+            e_rows[a] = work.tile([P, S], BF16, name="e_rows", tag="e_rows", bufs=3)
             row_sum[a] = work.tile([P, 1], F32, name="row_sum", tag="row_sum")
             nc.scalar.activation(
                 out=e_rows[a][:].rearrange("r (w p e) -> r w p e", w=2, e=2),
@@ -172,7 +169,7 @@ def tile_trimodalcrossattention_ver2_pa_e_kernel(tc, q, k, v, x, Wo_words, Wo_sc
         def reciprocal_square(a):
             recip = work.tile([P, 1], F32, name="recip", tag="recip")
             nc.vector.reciprocal(out=recip[:], in_=row_sum[a][:])
-            recip_sq[a] = work.tile([P, P], F32, name="recip_sq", tag="recip_sq")
+            recip_sq[a] = work.tile([P, P], F32, name="recip_sq", tag="recip_sq", bufs=3)
             nc.vector.tensor_copy(out=recip_sq[a][:], in_=recip[:].to_broadcast([P, P]))
 
         def regroup_values(m, g):
@@ -192,21 +189,17 @@ def tile_trimodalcrossattention_ver2_pa_e_kernel(tc, q, k, v, x, Wo_words, Wo_sc
 
         def sort_x(u):
             words = x_raw[u // TILES][:, u % TILES, :].bitcast(F32)
-            x_sorted[u] = work.tile([P, X_PASSES, 2, P], F32, name="x_sorted", tag="x_sorted")
-            nc.scalar.copy(out=x_sorted[u][:], in_=words.rearrange("r (g p w) -> r g w p", g=X_PASSES, w=2))
-
-        def transpose_x(u):
-            x_psum = psum.tile([P, X_PASSES, 2, P], F32, name="x_psum", tag="bank")
-            for g in range(X_PASSES):
-                for w in range(2):
-                    nc.tensor.transpose(x_psum[:, g, w, :], x_sorted[u][:, g, w, :], ident_f32[:])
-            return x_psum
+            x_sorted[u] = work.tile([P, 2 * X_PASSES, P], F32, name="x_sorted", tag="x_sorted")
+            nc.scalar.copy(
+                out=x_sorted[u][:].rearrange("r (g w) p -> r g w p", w=2),
+                in_=words.rearrange("r (g p w) -> r g w p", g=X_PASSES, w=2),
+            )
 
         def x_leaves_psum(x_psum):
             x_grouped = work.tile([P, X_PASSES * P * PACK], BF16, name="x_grouped", tag="x_grouped", align_bytes=64)
             nc.scalar.copy(
                 out=x_grouped[:].bitcast(F32).rearrange("p (g r w) -> p g r w", g=X_PASSES, w=2),
-                in_=x_psum[:].rearrange("p g w r -> p g r w"),
+                in_=x_psum[:].rearrange("p (g w) r -> p g r w", w=2),
             )
             return x_grouped
 
@@ -283,30 +276,39 @@ def tile_trimodalcrossattention_ver2_pa_e_kernel(tc, q, k, v, x, Wo_words, Wo_sc
         with tc.manual_schedule():
             load_tile_by_tile(k_raw, 0, k, "k_raw")
             load_tile_by_tile(q_raw, 0, q, "q_raw")
-            for step in range(-TILES, UNITS + 3):
-                u_scores, u_ctx, u_out = step, step - 2, step - 3
+            for step in range(-TILES, UNITS + 4):
+                u_scores, u_e, u_ctx, u_out = step, step - 2, step - 3, step - 4
                 if (step + 1) % TILES == 0 and step + 1 < UNITS:
                     load_modality((step + 1) // TILES)
-                if 0 <= u_ctx < UNITS:
-                    sort_x(u_ctx)
-                k_psum = scores_and_transposes(u_scores)
-                values_due = 0 <= u_scores < UNITS and u_scores % TILES < X_PASSES
-                if values_due:
-                    v_grouped = regroup_values(u_scores // TILES, u_scores % TILES)
-                if 0 <= u_ctx < UNITS:
-                    x_psum = transpose_x(u_ctx)
-                    x_grouped = x_leaves_psum(x_psum)
-                if k_psum is not None:
-                    keys_leave_psum(u_scores + TILES, k_psum)
-                if 0 <= u_ctx < UNITS:
+                filled = scores_and_transposes(u_scores)
+                if "q" in filled:
+                    queries_leave_psum(u_scores + 1, filled["q"])
+                if "x" in filled:
+                    x_grouped = x_leaves_psum(filled["x"])
+                if "scores" in filled:
+                    softmax_maximum(u_scores, filled["scores"])
+                if "er" in filled:
+                    e_grouped = e_and_reciprocal_leave_psum(u_e, filled["er"])
+                if "k" in filled:
+                    keys_leave_psum(u_scores + TILES, filled["k"])
+                if "scores" in filled:
+                    softmax_exponential(u_scores, filled["scores"])
+                if 0 <= u_ctx + 1 < UNITS:
+                    sort_x(u_ctx + 1)
+                if "x" in filled:
                     quantise_x(u_ctx, x_grouped)
-                if 0 <= u_scores < UNITS:
-                    reciprocal_square(u_scores)
-                if values_due:
-                    quantise_values(u_scores // TILES, u_scores % TILES, v_grouped)
+                if "er" in filled:
+                    quantise_e(u_e, e_grouped)
                 if 0 <= u_ctx < UNITS:
                     context_products(u_ctx)
                     normalise_and_quantise_context(u_ctx)
+                if "scores" in filled:
+                    reciprocal_square(u_scores)
+                values_due = "scores" in filled and u_scores % 2 == 0
+                if values_due:
+                    v_grouped = regroup_values(u_scores // TILES, (u_scores % TILES) // 2)
                 if 0 <= u_out < UNITS:
                     out_banks = output_products(u_out)
                     add_bias_and_store(u_out, out_banks)
+                if values_due:
+                    quantise_values(u_scores // TILES, (u_scores % TILES) // 2, v_grouped)

@@ -45,8 +45,9 @@ def tile_trimodalcrossattention_ver2_pa_e_kernel(tc, q, k, v, x, Wo_words, Wo_sc
 
         q_raw, k_raw, v_raw, x_raw, wo_words, bias = {}, {}, {}, {}, {}, {}
         kT, v_codes, v_plane = {}, {}, {}
-        qT, neg_max, e_rows, row_sum, recip_sq, recip_bc = {}, {}, {}, {}, {}, {}
+        qT, neg_max, e_rows, row_sum, recip_bc = {}, {}, {}, {}, {}
         e_codes, e_plane, comb_codes, comb_plane, ctx_psum, x_sorted = {}, {}, {}, {}, {}, {}
+        recip, comb_grouped = {}, {}
 
         def rows_on_partitions(dram_rows):
             return dram_rows.rearrange("(p i) n -> p i n", i=TILES)
@@ -65,41 +66,41 @@ def tile_trimodalcrossattention_ver2_pa_e_kernel(tc, q, k, v, x, Wo_words, Wo_sc
                 load_tile_by_tile(k_raw, m + 1, k, "k_raw")
             load_whole(v_raw, m, v[(m + 1) % MODS, 0], "v_raw")
             load_whole(x_raw, m, x[m, 0], "x_raw")
+            if m + 1 < MODS:
+                load_tile_by_tile(q_raw, m + 1, q, "q_raw")
             for quadrant in range(4):
                 nc.sync.dma_start(
                     out=wo_planes[32 * quadrant : 32 * quadrant + 16, m, :].bitcast(I32),
                     in_=Wo_scales[PASSES * m : PASSES * (m + 1), 4 * quadrant : 4 * quadrant + 4, :].bitcast(I32),
                 )
-            bias[m] = const.tile([P, D], BF16, name="bias%d" % m)
-            nc.sync.dma_start(out=bias[m][:], in_=bo[m].partition_broadcast(P))
             wo_words[m] = const.tile([P, PASSES, D], I32, name="wo_words%d" % m, align_bytes=64)
             for g in range(PASSES):
                 nc.sync.dma_start(
                     out=wo_words[m][:, g, :],
                     in_=Wo_words[PASSES * m + g].rearrange("p n t -> p (n t)").bitcast(I32),
                 )
-            if m + 1 < MODS:
-                load_tile_by_tile(q_raw, m + 1, q, "q_raw")
+            bias[m] = const.tile([P, D], BF16, name="bias%d" % m)
+            nc.sync.dma_start(out=bias[m][:], in_=bo[m].partition_broadcast(P))
 
         def scores_and_transposes(a):
             next_q, key_tile, u_e, u_x = a + 1, a + TILES, a - 2, a - 3
             filled = {}
-            if 0 <= a < UNITS:
-                filled["scores"] = psum.tile([P, S], F32, name="scores", tag="bank")
-                q_pairs = qT[a][:].rearrange("p c (r e) -> p c r e", e=2)
-                k_pairs = kT[a // TILES][:].rearrange("p c (r e) -> p c r e", e=2)
             if 0 <= next_q < UNITS:
                 filled["q"] = psum.tile([P, WORD_CHUNKS, P], F32, name="q_psum", tag="bank")
                 q_words = q_raw[next_q // TILES][:, next_q % TILES, :].bitcast(F32)
             if 0 <= u_x < UNITS:
                 filled["x"] = psum.tile([P, 2 * X_PASSES, P], F32, name="x_psum", tag="bank")
+            if 0 <= a < UNITS:
+                filled["scores"] = psum.tile([P, S], F32, name="scores", tag="bank")
+                q_pairs = qT[a][:].rearrange("p c (r e) -> p c r e", e=2)
+                k_pairs = kT[a // TILES][:].rearrange("p c (r e) -> p c r e", e=2)
             if 0 <= key_tile < UNITS:
                 filled["k"] = psum.tile([P, WORD_CHUNKS, P], F32, name="k_psum", tag="bank")
                 k_words = k_raw[key_tile // TILES][:, key_tile % TILES, :].bitcast(F32)
             if 0 <= u_e < UNITS:
                 filled["er"] = psum.tile([P, 3, P], F32, name="er_psum", tag="bank")
                 e_words = e_rows[u_e][:].bitcast(F32)
-                er_sources = [e_words[:, 0:P], e_words[:, P : 2 * P], recip_sq[u_e][:]]
+                er_sources = [e_words[:, 0:P], e_words[:, P : 2 * P], recip[u_e][:].to_broadcast([P, P])]
             for c in range(WORD_CHUNKS):
                 for e in range(2):
                     if 0 <= a < UNITS:
@@ -166,11 +167,9 @@ def tile_trimodalcrossattention_ver2_pa_e_kernel(tc, q, k, v, x, Wo_words, Wo_sc
                 accum_out=row_sum[a][:],
             )
 
-        def reciprocal_square(a):
-            recip = work.tile([P, 1], F32, name="recip", tag="recip")
-            nc.vector.reciprocal(out=recip[:], in_=row_sum[a][:])
-            recip_sq[a] = work.tile([P, P], F32, name="recip_sq", tag="recip_sq", bufs=3)
-            nc.vector.tensor_copy(out=recip_sq[a][:], in_=recip[:].to_broadcast([P, P]))
+        def reciprocal(a):
+            recip[a] = work.tile([P, 1], F32, name="recip", tag="recip", bufs=3)
+            nc.vector.reciprocal(out=recip[a][:], in_=row_sum[a][:])
 
         def regroup_values(m, g):
             grouped = work.tile([P, PACK * P * PACK], BF16, name="v_grouped", tag="v_grouped", align_bytes=64)
@@ -195,20 +194,11 @@ def tile_trimodalcrossattention_ver2_pa_e_kernel(tc, q, k, v, x, Wo_words, Wo_sc
                 in_=words.rearrange("r (g p w) -> r g w p", g=X_PASSES, w=2),
             )
 
-        def x_leaves_psum(x_psum):
-            x_grouped = work.tile([P, X_PASSES * P * PACK], BF16, name="x_grouped", tag="x_grouped", align_bytes=64)
+        def x_leaves_psum(u, x_psum):
+            comb_grouped[u] = work.tile([P, PASSES, P * PACK], BF16, name="comb_grouped", tag="comb_grouped", align_bytes=64)
             nc.scalar.copy(
-                out=x_grouped[:].bitcast(F32).rearrange("p (g r w) -> p g r w", g=X_PASSES, w=2),
+                out=comb_grouped[u][:, 0:X_PASSES, :].bitcast(F32).rearrange("p g (r w) -> p g r w", w=2),
                 in_=x_psum[:].rearrange("p (g w) r -> p g r w", w=2),
-            )
-            return x_grouped
-
-        def quantise_x(u, x_grouped):
-            comb_codes[u] = work.tile([P, PASSES * P], U32, name="comb_codes", tag="comb_codes", bufs=3, align_bytes=64)
-            comb_plane[u] = work.tile([P, PASSES * P], U8, name="comb_plane", tag="comb_plane", bufs=3, align_bytes=64)
-            cols = slice(0, X_PASSES * P)
-            nc.vector.quantize_mx(
-                out=comb_codes[u][:, cols].bitcast(FP8X4), scales=comb_plane[u][:, cols], in_=x_grouped[:]
             )
 
         def context_products(u):
@@ -229,24 +219,23 @@ def tile_trimodalcrossattention_ver2_pa_e_kernel(tc, q, k, v, x, Wo_words, Wo_sc
                     )
                 ctx_psum[u].append(bank)
 
-        def normalise_and_quantise_context(u):
-            grouped = []
+        def normalise_context(u):
             for g in range(X_PASSES):
-                ctx_grouped = work.tile([P, P, PACK], BF16, name="ctx_grouped", tag="ctx_grouped", align_bytes=64)
                 nc.vector.tensor_tensor(
-                    out=ctx_grouped[:],
+                    out=comb_grouped[u][:, X_PASSES + g, :].rearrange("p (r t) -> p r t", t=PACK),
                     in0=ctx_psum[u][g][:].rearrange("p t r -> p r t"),
                     in1=recip_bc[u][:].unsqueeze(2).to_broadcast([P, P, PACK]),
                     op=ALU.mult,
                 )
-                grouped.append(ctx_grouped)
-            for g in range(X_PASSES):
-                cols = slice(P * (X_PASSES + g), P * (X_PASSES + g + 1))
-                nc.vector.quantize_mx(
-                    out=comb_codes[u][:, cols].bitcast(FP8X4),
-                    scales=comb_plane[u][:, cols],
-                    in_=grouped[g][:].rearrange("p r t -> p (r t)"),
-                )
+
+        def quantise_concatenation(u):
+            comb_codes[u] = work.tile([P, PASSES * P], U32, name="comb_codes", tag="comb_codes", align_bytes=64)
+            comb_plane[u] = work.tile([P, PASSES * P], U8, name="comb_plane", tag="comb_plane", align_bytes=64)
+            nc.vector.quantize_mx(
+                out=comb_codes[u][:].bitcast(FP8X4),
+                scales=comb_plane[u][:],
+                in_=comb_grouped[u][:].rearrange("p g c -> p (g c)"),
+            )
 
         def output_products(u):
             m = u // TILES
@@ -280,35 +269,35 @@ def tile_trimodalcrossattention_ver2_pa_e_kernel(tc, q, k, v, x, Wo_words, Wo_sc
                 u_scores, u_e, u_ctx, u_out = step, step - 2, step - 3, step - 4
                 if (step + 1) % TILES == 0 and step + 1 < UNITS:
                     load_modality((step + 1) // TILES)
+                regrouped = u_scores - 1
+                if 0 <= regrouped < UNITS and regrouped % TILES < X_PASSES:
+                    quantise_values(regrouped // TILES, regrouped % TILES, v_grouped)
                 filled = scores_and_transposes(u_scores)
                 if "q" in filled:
                     queries_leave_psum(u_scores + 1, filled["q"])
                 if "x" in filled:
-                    x_grouped = x_leaves_psum(filled["x"])
+                    x_leaves_psum(u_ctx, filled["x"])
+                if 0 <= u_ctx + 1 < UNITS:
+                    sort_x(u_ctx + 1)
                 if "scores" in filled:
                     softmax_maximum(u_scores, filled["scores"])
+                if "scores" in filled and u_scores % TILES < X_PASSES:
+                    v_grouped = regroup_values(u_scores // TILES, u_scores % TILES)
                 if "er" in filled:
                     e_grouped = e_and_reciprocal_leave_psum(u_e, filled["er"])
                 if "k" in filled:
                     keys_leave_psum(u_scores + TILES, filled["k"])
                 if "scores" in filled:
                     softmax_exponential(u_scores, filled["scores"])
-                if 0 <= u_ctx + 1 < UNITS:
-                    sort_x(u_ctx + 1)
-                if "x" in filled:
-                    quantise_x(u_ctx, x_grouped)
                 if "er" in filled:
                     quantise_e(u_e, e_grouped)
                 if 0 <= u_ctx < UNITS:
                     context_products(u_ctx)
-                    normalise_and_quantise_context(u_ctx)
+                    normalise_context(u_ctx)
                 if "scores" in filled:
-                    reciprocal_square(u_scores)
-                values_due = "scores" in filled and u_scores % 2 == 0
-                if values_due:
-                    v_grouped = regroup_values(u_scores // TILES, (u_scores % TILES) // 2)
+                    reciprocal(u_scores)
+                if 0 <= u_ctx < UNITS:
+                    quantise_concatenation(u_ctx)
                 if 0 <= u_out < UNITS:
                     out_banks = output_products(u_out)
                     add_bias_and_store(u_out, out_banks)
-                if values_due:
-                    quantise_values(u_scores // TILES, (u_scores % TILES) // 2, v_grouped)

@@ -45,16 +45,17 @@ def tile_trimodalcrossattention_ver2_pa_e_kernel(tc, q, k, v, x, Wo_words, Wo_sc
 
         q_raw, k_raw, v_raw, x_raw, wo_words, bias = {}, {}, {}, {}, {}, {}
         kT, v_codes, v_plane = {}, {}, {}
-        qT, neg_max, e_rows, row_sum, recip_bc = {}, {}, {}, {}, {}
+        qT, row_max, e_rows, row_sum, recip_bc = {}, {}, {}, {}, {}
         e_codes, e_plane, comb_codes, comb_plane, ctx_psum, x_sorted = {}, {}, {}, {}, {}, {}
-        recip, comb_grouped = {}, {}
+        recip, comb_grouped, v_grouped = {}, {}, {}
 
         def rows_on_partitions(dram_rows):
             return dram_rows.rearrange("(p i) n -> p i n", i=TILES)
 
-        def load_tile_by_tile(table, m, dram, name):
-            table[m] = loads.tile([P, TILES, D], BF16, name=name, tag=name)
-            for i in range(TILES):
+        def load_tile_by_tile(table, m, dram, name, tiles):
+            if m not in table:
+                table[m] = loads.tile([P, TILES, D], BF16, name=name, tag=name)
+            for i in tiles:
                 nc.sync.dma_start(out=table[m][:, i, :], in_=rows_on_partitions(dram[m, 0])[:, i, :])
 
         def load_whole(table, m, dram_rows, name):
@@ -63,11 +64,13 @@ def tile_trimodalcrossattention_ver2_pa_e_kernel(tc, q, k, v, x, Wo_words, Wo_sc
 
         def load_modality(m):
             if m + 1 < MODS:
-                load_tile_by_tile(k_raw, m + 1, k, "k_raw")
+                load_tile_by_tile(k_raw, m + 1, k, "k_raw", range(0, 1))
             load_whole(v_raw, m, v[(m + 1) % MODS, 0], "v_raw")
+            if m + 1 < MODS:
+                load_tile_by_tile(k_raw, m + 1, k, "k_raw", range(1, TILES))
             load_whole(x_raw, m, x[m, 0], "x_raw")
             if m + 1 < MODS:
-                load_tile_by_tile(q_raw, m + 1, q, "q_raw")
+                load_tile_by_tile(q_raw, m + 1, q, "q_raw", range(TILES))
             for quadrant in range(4):
                 nc.sync.dma_start(
                     out=wo_planes[32 * quadrant : 32 * quadrant + 16, m, :].bitcast(I32),
@@ -150,19 +153,19 @@ def tile_trimodalcrossattention_ver2_pa_e_kernel(tc, q, k, v, x, Wo_words, Wo_sc
 
 
         def softmax_maximum(a, scores):
-            row_max = work.tile([P, 1], F32, name="row_max", tag="row_max")
-            nc.vector.tensor_reduce(out=row_max[:], in_=scores[:], axis=AXIS.X, op=ALU.max)
-            neg_max[a] = work.tile([P, 1], F32, name="neg_max", tag="neg_max")
-            nc.vector.tensor_scalar(out=neg_max[a][:], in0=row_max[:], scalar1=-SCALE, scalar2=None, op0=ALU.mult)
+            row_max[a] = work.tile([P, 1], F32, name="row_max", tag="row_max")
+            nc.vector.tensor_reduce(out=row_max[a][:], in_=scores[:], axis=AXIS.X, op=ALU.max)
 
         def softmax_exponential(a, scores):
+            neg_max = work.tile([P, 1], F32, name="neg_max", tag="neg_max")
+            nc.scalar.mul(out=neg_max[:], in_=row_max[a][:], mul=-SCALE)
             e_rows[a] = work.tile([P, S], BF16, name="e_rows", tag="e_rows", bufs=3)
             row_sum[a] = work.tile([P, 1], F32, name="row_sum", tag="row_sum")
             nc.scalar.activation(
                 out=e_rows[a][:].rearrange("r (w p e) -> r w p e", w=2, e=2),
                 in_=scores[:].rearrange("r (w e p) -> r w p e", w=2, e=2),
                 func=ACT.Exp,
-                bias=neg_max[a][:],
+                bias=neg_max[:],
                 scale=SCALE,
                 accum_out=row_sum[a][:],
             )
@@ -172,23 +175,25 @@ def tile_trimodalcrossattention_ver2_pa_e_kernel(tc, q, k, v, x, Wo_words, Wo_sc
             nc.vector.reciprocal(out=recip[a][:], in_=row_sum[a][:])
 
         def regroup_values(m, g):
-            grouped = work.tile([P, PACK * P * PACK], BF16, name="v_grouped", tag="v_grouped", align_bytes=64)
+            if g == 0:
+                v_grouped[m] = work.tile([P, X_PASSES, HALF * PACK], BF16, name="v_grouped", tag="v_grouped", align_bytes=64)
             nc.vector.tensor_copy(
-                out=grouped[:].rearrange("p (t r j) -> p r j t", t=PACK, j=PACK),
+                out=v_grouped[m][:, g, :].rearrange("p (t r j) -> p r j t", t=PACK, j=PACK),
                 in_=v_raw[m][:, :, HALF * g : HALF * (g + 1)].rearrange("p j (r t) -> p r j t", t=PACK),
             )
-            return grouped
 
-        def quantise_values(m, g, grouped):
-            if g == 0:
-                v_codes[m] = work.tile([P, D], U32, name="v_codes", tag="v_codes", align_bytes=64)
-                v_plane[m] = work.tile([P, D], U8, name="v_plane", tag="v_plane", align_bytes=64)
-            cols = slice(HALF * g, HALF * (g + 1))
-            nc.vector.quantize_mx(out=v_codes[m][:, cols].bitcast(FP8X4), scales=v_plane[m][:, cols], in_=grouped[:])
+        def quantise_values(m):
+            v_codes[m] = work.tile([P, D], U32, name="v_codes", tag="v_codes", align_bytes=64)
+            v_plane[m] = work.tile([P, D], U8, name="v_plane", tag="v_plane", align_bytes=64)
+            nc.vector.quantize_mx(
+                out=v_codes[m][:].bitcast(FP8X4),
+                scales=v_plane[m][:],
+                in_=v_grouped[m][:].rearrange("p g c -> p (g c)"),
+            )
 
         def sort_x(u):
             words = x_raw[u // TILES][:, u % TILES, :].bitcast(F32)
-            x_sorted[u] = work.tile([P, 2 * X_PASSES, P], F32, name="x_sorted", tag="x_sorted")
+            x_sorted[u] = work.tile([P, 2 * X_PASSES, P], F32, name="x_sorted", tag="x_sorted", bufs=3)
             nc.scalar.copy(
                 out=x_sorted[u][:].rearrange("r (g w) p -> r g w p", w=2),
                 in_=words.rearrange("r (g p w) -> r g w p", g=X_PASSES, w=2),
@@ -263,32 +268,31 @@ def tile_trimodalcrossattention_ver2_pa_e_kernel(tc, q, k, v, x, Wo_words, Wo_sc
                 nc.sync.dma_start(out=rows_on_partitions(out[m, 0])[:, i, cols], in_=result[:])
 
         with tc.manual_schedule():
-            load_tile_by_tile(k_raw, 0, k, "k_raw")
-            load_tile_by_tile(q_raw, 0, q, "q_raw")
+            load_tile_by_tile(k_raw, 0, k, "k_raw", range(TILES))
+            load_tile_by_tile(q_raw, 0, q, "q_raw", range(TILES))
             for step in range(-TILES, UNITS + 4):
                 u_scores, u_e, u_ctx, u_out = step, step - 2, step - 3, step - 4
                 if (step + 1) % TILES == 0 and step + 1 < UNITS:
                     load_modality((step + 1) // TILES)
-                regrouped = u_scores - 1
-                if 0 <= regrouped < UNITS and regrouped % TILES < X_PASSES:
-                    quantise_values(regrouped // TILES, regrouped % TILES, v_grouped)
                 filled = scores_and_transposes(u_scores)
                 if "q" in filled:
                     queries_leave_psum(u_scores + 1, filled["q"])
                 if "x" in filled:
                     x_leaves_psum(u_ctx, filled["x"])
-                if 0 <= u_ctx + 1 < UNITS:
-                    sort_x(u_ctx + 1)
                 if "scores" in filled:
                     softmax_maximum(u_scores, filled["scores"])
                 if "scores" in filled and u_scores % TILES < X_PASSES:
-                    v_grouped = regroup_values(u_scores // TILES, u_scores % TILES)
+                    regroup_values(u_scores // TILES, u_scores % TILES)
+                if "scores" in filled and u_scores % TILES == X_PASSES:
+                    quantise_values(u_scores // TILES)
                 if "er" in filled:
                     e_grouped = e_and_reciprocal_leave_psum(u_e, filled["er"])
                 if "k" in filled:
                     keys_leave_psum(u_scores + TILES, filled["k"])
                 if "scores" in filled:
                     softmax_exponential(u_scores, filled["scores"])
+                if 0 <= u_ctx + 2 < UNITS:
+                    sort_x(u_ctx + 2)
                 if "er" in filled:
                     quantise_e(u_e, e_grouped)
                 if 0 <= u_ctx < UNITS:

@@ -104,26 +104,35 @@ def tile_trimodalcrossattention_ver2_pa_e_kernel(tc, q, k, v, x, Wo_words, Wo_sc
                 filled["er"] = psum.tile([P, 3, P], F32, name="er_psum", tag="bank")
                 e_words = e_rows[u_e][:].bitcast(F32)
                 er_sources = [e_words[:, 0:P], e_words[:, P : 2 * P], recip[u_e][:].to_broadcast([P, P])]
-            for c in range(WORD_CHUNKS):
-                for e in range(2):
-                    if 0 <= a < UNITS:
-                        nc.tensor.matmul(
-                            out=filled["scores"][:],
-                            lhsT=q_pairs[:, c, :, e],
-                            rhs=k_pairs[:, c, :, e],
-                            start=(c == 0 and e == 0),
-                            stop=(c == WORD_CHUNKS - 1 and e == 1),
-                        )
-                    turn = 2 * c + e
-                    late = turn - WORD_CHUNKS
-                    if late < 0 and 0 <= next_q < UNITS:
-                        nc.tensor.transpose(filled["q"][:, turn, :], q_words[:, P * turn : P * (turn + 1)], ident_f32[:])
-                    if late < 0 and 0 <= u_x < UNITS:
-                        nc.tensor.transpose(filled["x"][:, turn, :], x_sorted[u_x][:, turn, :], ident_f32[:])
-                    if late >= 0 and 0 <= key_tile < UNITS:
-                        nc.tensor.transpose(filled["k"][:, late, :], k_words[:, P * late : P * (late + 1)], ident_f32[:])
-                    if 0 <= late < 3 and 0 <= u_e < UNITS:
-                        nc.tensor.transpose(filled["er"][:, late, :], er_sources[late], ident_f32[:])
+            moves = []
+            for j in range(WORD_CHUNKS):
+                if 0 <= next_q < UNITS:
+                    moves.append((filled["q"][:, j, :], q_words[:, P * j : P * (j + 1)]))
+                if 0 <= u_x < UNITS:
+                    moves.append((filled["x"][:, j, :], x_sorted[u_x][:, j, :]))
+            for j in range(WORD_CHUNKS):
+                if 0 <= key_tile < UNITS:
+                    moves.append((filled["k"][:, j, :], k_words[:, P * j : P * (j + 1)]))
+                if j < 3 and 0 <= u_e < UNITS:
+                    moves.append((filled["er"][:, j, :], er_sources[j]))
+            products = [(c, e) for c in range(WORD_CHUNKS) for e in range(2)] if 0 <= a < UNITS else []
+            gaps = len(products) - 1
+            placed = 0
+            for n, (c, e) in enumerate(products):
+                nc.tensor.matmul(
+                    out=filled["scores"][:],
+                    lhsT=q_pairs[:, c, :, e],
+                    rhs=k_pairs[:, c, :, e],
+                    start=(n == 0),
+                    stop=(n == gaps),
+                )
+                if n < gaps:
+                    upto = (len(moves) * (n + 1) + gaps - 1) // gaps
+                    for target, source in moves[placed:upto]:
+                        nc.tensor.transpose(target, source, ident_f32[:])
+                    placed = upto
+            for target, source in moves[placed:]:
+                nc.tensor.transpose(target, source, ident_f32[:])
             return filled
 
         def queries_leave_psum(u, q_psum):

@@ -24,6 +24,9 @@ WORD_CHUNKS = D // (2 * P)
 HALF = 512
 X_PASSES = D // (P * PACK)
 PASSES = 2 * X_PASSES
+AHEAD = 4
+V_NEED = 0
+X_NEED = 1
 SCALE = 1.0 / 32.0
 
 FLOPS = 2 * MODS * (S * S * D + S * S * D + S * 2 * D * D)
@@ -62,15 +65,7 @@ def tile_trimodalcrossattention_ver2_pa_e_kernel(tc, q, k, v, x, Wo_words, Wo_sc
             table[m] = loads.tile([P, TILES, D], BF16, name=name, tag=name)
             nc.sync.dma_start(out=table[m][:], in_=rows_on_partitions(dram_rows))
 
-        def load_modality(m):
-            if m + 1 < MODS:
-                load_tile_by_tile(k_raw, m + 1, k, "k_raw", range(0, 1))
-            load_whole(v_raw, m, v[(m + 1) % MODS, 0], "v_raw")
-            if m + 1 < MODS:
-                load_tile_by_tile(k_raw, m + 1, k, "k_raw", range(1, TILES))
-            load_whole(x_raw, m, x[m, 0], "x_raw")
-            if m + 1 < MODS:
-                load_tile_by_tile(q_raw, m + 1, q, "q_raw", range(TILES))
+        def load_weights(m):
             for quadrant in range(4):
                 nc.sync.dma_start(
                     out=wo_planes[32 * quadrant : 32 * quadrant + 16, m, :].bitcast(I32),
@@ -85,7 +80,31 @@ def tile_trimodalcrossattention_ver2_pa_e_kernel(tc, q, k, v, x, Wo_words, Wo_sc
             bias[m] = const.tile([P, D], BF16, name="bias%d" % m)
             nc.sync.dma_start(out=bias[m][:], in_=bo[m].partition_broadcast(P))
 
-        def scores_and_transposes(a):
+        plan = []
+        for m in range(MODS):
+            for i in range(TILES):
+                plan.append((TILES * m + i - 1, 0, "q", m, i))
+                plan.append((max(TILES * m + i - TILES, -1), 1, "k", m, i))
+            plan.append((TILES * m + V_NEED, 2, "v", m, 0))
+            plan.append((TILES * m + X_NEED, 3, "x", m, 0))
+            plan.append((TILES * m + TILES, 4, "w", m, 0))
+        plan = sorted(plan)
+
+        def issue_loads(step):
+            while len(plan) > 0 and plan[0][0] <= step + AHEAD:
+                what, m, i = plan.pop(0)[2:]
+                if what == "q":
+                    load_tile_by_tile(q_raw, m, q, "q_raw", range(i, i + 1))
+                if what == "k":
+                    load_tile_by_tile(k_raw, m, k, "k_raw", range(i, i + 1))
+                if what == "v":
+                    load_whole(v_raw, m, v[(m + 1) % MODS, 0], "v_raw")
+                if what == "x":
+                    load_whole(x_raw, m, x[m, 0], "x_raw")
+                if what == "w":
+                    load_weights(m)
+
+        def scores_and_transposes(a, first_scores):
             next_q, key_tile, u_e, u_x = a + 1, a + TILES, a - 2, a - 3
             filled = {}
             if 0 <= next_q < UNITS:
@@ -93,10 +112,13 @@ def tile_trimodalcrossattention_ver2_pa_e_kernel(tc, q, k, v, x, Wo_words, Wo_sc
                 q_words = q_raw[next_q // TILES][:, next_q % TILES, :].bitcast(F32)
             if 0 <= u_x < UNITS:
                 filled["x"] = psum.tile([P, 2 * X_PASSES, P], F32, name="x_psum", tag="bank")
-            if 0 <= a < UNITS:
+            if a == 0:
+                filled["scores"] = first_scores
+            if 0 < a < UNITS:
                 filled["scores"] = psum.tile([P, S], F32, name="scores", tag="bank")
+            if 0 <= a < UNITS:
                 q_pairs = qT[a][:].rearrange("p c (r e) -> p c r e", e=2)
-                k_pairs = kT[a // TILES][:].rearrange("p c (r e) -> p c r e", e=2)
+                k_pairs = kT[a // TILES][:].rearrange("p i c (r e) -> p i c r e", e=2)
             if 0 <= key_tile < UNITS:
                 filled["k"] = psum.tile([P, WORD_CHUNKS, P], F32, name="k_psum", tag="bank")
                 k_words = k_raw[key_tile // TILES][:, key_tile % TILES, :].bitcast(F32)
@@ -119,10 +141,11 @@ def tile_trimodalcrossattention_ver2_pa_e_kernel(tc, q, k, v, x, Wo_words, Wo_sc
             gaps = len(products) - 1
             placed = 0
             for n, (c, e) in enumerate(products):
+                tiles = slice(TILES - 1, TILES) if a == 0 else slice(0, TILES)
                 nc.tensor.matmul(
-                    out=filled["scores"][:],
+                    out=filled["scores"][:].rearrange("p (i r) -> p i r", r=P)[:, tiles, :],
                     lhsT=q_pairs[:, c, :, e],
-                    rhs=k_pairs[:, c, :, e],
+                    rhs=k_pairs[:, tiles, c, :, e],
                     start=(n == 0),
                     stop=(n == gaps),
                 )
@@ -134,6 +157,34 @@ def tile_trimodalcrossattention_ver2_pa_e_kernel(tc, q, k, v, x, Wo_words, Wo_sc
             for target, source in moves[placed:]:
                 nc.tensor.transpose(target, source, ident_f32[:])
             return filled
+
+        def first_unit():
+            q_psum = psum.tile([P, WORD_CHUNKS, P], F32, name="q_psum", tag="bank")
+            q_words = q_raw[0][:, 0, :].bitcast(F32)
+            for j in range(WORD_CHUNKS):
+                nc.tensor.transpose(q_psum[:, j, :], q_words[:, P * j : P * (j + 1)], ident_f32[:])
+            queries_leave_psum(0, q_psum)
+            for i in range(TILES):
+                k_psum = psum.tile([P, WORD_CHUNKS, P], F32, name="k_psum", tag="bank")
+                k_words = k_raw[0][:, i, :].bitcast(F32)
+                for j in range(WORD_CHUNKS):
+                    nc.tensor.transpose(k_psum[:, j, :], k_words[:, P * j : P * (j + 1)], ident_f32[:])
+                keys_leave_psum(i, k_psum)
+                if i == 1:
+                    scores = psum.tile([P, S], F32, name="scores", tag="bank")
+                if i > 0:
+                    q_pairs = qT[0][:].rearrange("p c (r e) -> p c r e", e=2)
+                    k_pairs = kT[0][:].rearrange("p i c (r e) -> p i c r e", e=2)
+                    for c in range(WORD_CHUNKS):
+                        for e in range(2):
+                            nc.tensor.matmul(
+                                out=scores[:, P * (i - 1) : P * i],
+                                lhsT=q_pairs[:, c, :, e],
+                                rhs=k_pairs[:, i - 1, c, :, e],
+                                start=(c == 0 and e == 0),
+                                stop=(c == WORD_CHUNKS - 1 and e == 1),
+                            )
+            return scores
 
         def queries_leave_psum(u, q_psum):
             qT[u] = work.tile([P, WORD_CHUNKS, 2 * P], BF16, name="qT", tag="qT")
@@ -157,8 +208,8 @@ def tile_trimodalcrossattention_ver2_pa_e_kernel(tc, q, k, v, x, Wo_words, Wo_sc
         def keys_leave_psum(key_tile, k_psum):
             m, i = key_tile // TILES, key_tile % TILES
             if i == 0:
-                kT[m] = work.tile([P, WORD_CHUNKS, 2 * S], BF16, name="kT", tag="kT")
-            nc.scalar.copy(out=kT[m][:].bitcast(F32)[:, :, P * i : P * (i + 1)], in_=k_psum[:])
+                kT[m] = work.tile([P, TILES, WORD_CHUNKS, 2 * P], BF16, name="kT", tag="kT")
+            nc.scalar.copy(out=kT[m][:, i, :, :].bitcast(F32), in_=k_psum[:])
 
 
         def softmax_maximum(a, scores):
@@ -272,18 +323,17 @@ def tile_trimodalcrossattention_ver2_pa_e_kernel(tc, q, k, v, x, Wo_words, Wo_sc
             m, i = u // TILES, u % TILES
             for h in range(D // HALF):
                 cols = slice(HALF * h, HALF * (h + 1))
-                result = work.tile([P, HALF], F32, name="result", tag="result", bufs=4)
+                result = work.tile([P, HALF], F32, name="result", tag="result", bufs=6)
                 nc.vector.tensor_tensor(out=result[:], in0=banks[h][:], in1=bias[m][:, cols], op=ALU.add)
                 nc.sync.dma_start(out=rows_on_partitions(out[m, 0])[:, i, cols], in_=result[:])
 
         with tc.manual_schedule():
-            load_tile_by_tile(k_raw, 0, k, "k_raw", range(TILES))
-            load_tile_by_tile(q_raw, 0, q, "q_raw", range(TILES))
-            for step in range(-TILES, UNITS + 4):
+            issue_loads(-1)
+            first_scores = first_unit()
+            for step in range(0, UNITS + 4):
                 u_scores, u_e, u_ctx, u_out = step, step - 2, step - 3, step - 4
-                if (step + 1) % TILES == 0 and step + 1 < UNITS:
-                    load_modality((step + 1) // TILES)
-                filled = scores_and_transposes(u_scores)
+                issue_loads(step)
+                filled = scores_and_transposes(u_scores, first_scores)
                 if "q" in filled:
                     queries_leave_psum(u_scores + 1, filled["q"])
                 if "x" in filled:

@@ -43,7 +43,7 @@ def tile_trimodalcrossattention_ver2_pa_e_kernel(tc, q, k, v, x, Wo_words, Wo_sc
         ident_f32 = const.tile([P, P], F32, name="ident_f32")
         make_identity(nc, ident_f32[:])
 
-        wo_planes = const.tile([P, MODS, D], U8, name="wo_planes", align_bytes=64)
+        wo_planes = const.tile([P, MODS, D], U8, name="wo_planes", align_bytes=256)
         nc.vector.memset(wo_planes[:].rearrange("p m n -> p (m n)").bitcast(I32), 0)
 
         q_raw, k_raw, v_raw, x_raw, wo_words, bias = {}, {}, {}, {}, {}, {}
@@ -71,7 +71,7 @@ def tile_trimodalcrossattention_ver2_pa_e_kernel(tc, q, k, v, x, Wo_words, Wo_sc
                     out=wo_planes[32 * quadrant : 32 * quadrant + 16, m, :].bitcast(I32),
                     in_=Wo_scales[PASSES * m : PASSES * (m + 1), 4 * quadrant : 4 * quadrant + 4, :].bitcast(I32),
                 )
-            wo_words[m] = const.tile([P, PASSES, D], I32, name="wo_words%d" % m, align_bytes=64)
+            wo_words[m] = const.tile([P, PASSES, D], I32, name="wo_words%d" % m, align_bytes=256)
             for g in range(PASSES):
                 nc.sync.dma_start(
                     out=wo_words[m][:, g, :],
@@ -191,7 +191,7 @@ def tile_trimodalcrossattention_ver2_pa_e_kernel(tc, q, k, v, x, Wo_words, Wo_sc
             nc.scalar.copy(out=qT[u][:].bitcast(F32), in_=q_psum[:])
 
         def e_and_reciprocal_leave_psum(u, er_psum):
-            e_grouped = work.tile([P, P * PACK], BF16, name="e_grouped", tag="e_grouped", align_bytes=64)
+            e_grouped = work.tile([P, P * PACK], BF16, name="e_grouped", tag="e_grouped", align_bytes=256)
             nc.scalar.copy(
                 out=e_grouped[:].bitcast(F32).rearrange("p (r w) -> p r w", w=2),
                 in_=er_psum[:, 0:2, :].rearrange("p w r -> p r w"),
@@ -201,8 +201,8 @@ def tile_trimodalcrossattention_ver2_pa_e_kernel(tc, q, k, v, x, Wo_words, Wo_sc
             return e_grouped
 
         def quantise_e(u, e_grouped):
-            e_codes[u] = work.tile([P, P], U32, name="e_codes", tag="e_codes", align_bytes=64)
-            e_plane[u] = work.tile([P, P], U8, name="e_plane", tag="e_plane", align_bytes=64)
+            e_codes[u] = work.tile([P, P], U32, name="e_codes", tag="e_codes", align_bytes=256)
+            e_plane[u] = work.tile([P, P], U8, name="e_plane", tag="e_plane", align_bytes=256)
             nc.vector.quantize_mx(out=e_codes[u][:].bitcast(FP8X4), scales=e_plane[u][:], in_=e_grouped[:])
 
         def keys_leave_psum(key_tile, k_psum):
@@ -236,15 +236,15 @@ def tile_trimodalcrossattention_ver2_pa_e_kernel(tc, q, k, v, x, Wo_words, Wo_sc
 
         def regroup_values(m, g):
             if g == 0:
-                v_grouped[m] = work.tile([P, X_PASSES, HALF * PACK], BF16, name="v_grouped", tag="v_grouped", align_bytes=64)
+                v_grouped[m] = work.tile([P, X_PASSES, HALF * PACK], BF16, name="v_grouped", tag="v_grouped", align_bytes=256)
             nc.vector.tensor_copy(
                 out=v_grouped[m][:, g, :].rearrange("p (t r j) -> p r j t", t=PACK, j=PACK),
                 in_=v_raw[m][:, :, HALF * g : HALF * (g + 1)].rearrange("p j (r t) -> p r j t", t=PACK),
             )
 
         def quantise_values(m):
-            v_codes[m] = work.tile([P, D], U32, name="v_codes", tag="v_codes", align_bytes=64)
-            v_plane[m] = work.tile([P, D], U8, name="v_plane", tag="v_plane", align_bytes=64)
+            v_codes[m] = work.tile([P, D], U32, name="v_codes", tag="v_codes", align_bytes=256)
+            v_plane[m] = work.tile([P, D], U8, name="v_plane", tag="v_plane", align_bytes=256)
             nc.vector.quantize_mx(
                 out=v_codes[m][:].bitcast(FP8X4),
                 scales=v_plane[m][:],
@@ -260,7 +260,7 @@ def tile_trimodalcrossattention_ver2_pa_e_kernel(tc, q, k, v, x, Wo_words, Wo_sc
             )
 
         def x_leaves_psum(u, x_psum):
-            comb_grouped[u] = work.tile([P, PASSES, P * PACK], BF16, name="comb_grouped", tag="comb_grouped", align_bytes=64)
+            comb_grouped[u] = work.tile([P, PASSES, P * PACK], BF16, name="comb_grouped", tag="comb_grouped", align_bytes=256)
             nc.scalar.copy(
                 out=comb_grouped[u][:, 0:X_PASSES, :].bitcast(F32).rearrange("p g (r w) -> p g r w", w=2),
                 in_=x_psum[:].rearrange("p (g w) r -> p g r w", w=2),
@@ -294,8 +294,8 @@ def tile_trimodalcrossattention_ver2_pa_e_kernel(tc, q, k, v, x, Wo_words, Wo_sc
                 )
 
         def quantise_concatenation(u):
-            comb_codes[u] = work.tile([P, PASSES * P], U32, name="comb_codes", tag="comb_codes", align_bytes=64)
-            comb_plane[u] = work.tile([P, PASSES * P], U8, name="comb_plane", tag="comb_plane", align_bytes=64)
+            comb_codes[u] = work.tile([P, PASSES * P], U32, name="comb_codes", tag="comb_codes", align_bytes=256)
+            comb_plane[u] = work.tile([P, PASSES * P], U8, name="comb_plane", tag="comb_plane", align_bytes=256)
             nc.vector.quantize_mx(
                 out=comb_codes[u][:].bitcast(FP8X4),
                 scales=comb_plane[u][:],

from contextlib import ExitStack

import concourse.mybir as mybir
from concourse.masks import make_identity

BF16 = mybir.dt.bfloat16
F32 = mybir.dt.float32
I32 = mybir.dt.int32
U32 = mybir.dt.uint32
U8 = mybir.dt.uint8
FP8X4 = mybir.dt.float8_e4m3fn_x4
ACT = mybir.ActivationFunctionType
ALU = mybir.AluOpType
AXIS = mybir.AxisListType

P = 128
PACK = 4
MODS = 3
S = 512
D = 1024
TILES = S // P
UNITS = MODS * TILES
WORD_CHUNKS = D // (2 * P)
HALF = 512
X_PASSES = D // (P * PACK)
PASSES = 2 * X_PASSES
AHEAD = 4
V_NEED = 0
X_NEED = 1
SCALE = 1.0 / 32.0

FLOPS = 2 * MODS * (S * S * D + S * S * D + S * 2 * D * D)


def tile_trimodalcrossattention_ver2_pa_e_kernel(tc, q, k, v, x, Wo_words, Wo_scales, bo, out):
    nc = tc.nc
    with ExitStack() as stack:
        const = stack.enter_context(tc.tile_pool(name="const", bufs=1))
        loads = stack.enter_context(tc.tile_pool(name="loads", bufs=2))
        work = stack.enter_context(tc.tile_pool(name="work", bufs=2))
        psum = stack.enter_context(tc.psum_pool(name="psum", bufs=8))

        ident_f32 = const.tile([P, P], F32, name="ident_f32")
        make_identity(nc, ident_f32[:])

        wo_planes = const.tile([P, MODS, D], U8, name="wo_planes", align_bytes=256)
        nc.vector.memset(wo_planes[:].rearrange("p m n -> p (m n)").bitcast(I32), 0)

        q_raw, k_raw, v_raw, x_raw, wo_words, bias = {}, {}, {}, {}, {}, {}
        kT, v_codes, v_plane = {}, {}, {}
        qT, row_max, e_rows, row_sum, recip_bc = {}, {}, {}, {}, {}
        e_codes, e_plane, comb_codes, comb_plane, ctx_psum, x_sorted = {}, {}, {}, {}, {}, {}
        recip, comb_grouped, v_grouped = {}, {}, {}

        def rows_on_partitions(dram_rows):
            return dram_rows.rearrange("(p i) n -> p i n", i=TILES)

        def load_tile_by_tile(table, m, dram, name, tiles):
            if m not in table:
                table[m] = loads.tile([P, TILES, D], BF16, name=name, tag=name)
            for i in tiles:
                nc.sync.dma_start(out=table[m][:, i, :], in_=rows_on_partitions(dram[m, 0])[:, i, :])

        def load_whole(table, m, dram_rows, name):
            table[m] = loads.tile([P, TILES, D], BF16, name=name, tag=name)
            nc.sync.dma_start(out=table[m][:], in_=rows_on_partitions(dram_rows))

        def load_weights(m):
            for quadrant in range(4):
                nc.sync.dma_start(
                    out=wo_planes[32 * quadrant : 32 * quadrant + 16, m, :].bitcast(I32),
                    in_=Wo_scales[PASSES * m : PASSES * (m + 1), 4 * quadrant : 4 * quadrant + 4, :].bitcast(I32),
                )
            wo_words[m] = const.tile([P, PASSES, D], I32, name="wo_words%d" % m, align_bytes=256)
            for g in range(PASSES):
                nc.sync.dma_start(
                    out=wo_words[m][:, g, :],
                    in_=Wo_words[PASSES * m + g].rearrange("p n t -> p (n t)").bitcast(I32),
                )
            bias[m] = const.tile([P, D], BF16, name="bias%d" % m)
            nc.sync.dma_start(out=bias[m][:], in_=bo[m].partition_broadcast(P))

        plan = []
        for m in range(MODS):
            for i in range(TILES):
                plan.append((TILES * m + i - 1, 0, "q", m, i))
                plan.append((max(TILES * m + i - TILES, -1), 1, "k", m, i))
            plan.append((TILES * m + V_NEED, 2, "v", m, 0))
            plan.append((TILES * m + X_NEED, 3, "x", m, 0))
            plan.append((TILES * m + TILES, 4, "w", m, 0))
        plan = sorted(plan)

        def issue_loads(step):
            while len(plan) > 0 and plan[0][0] <= step + AHEAD:
                what, m, i = plan.pop(0)[2:]
                if what == "q":
                    load_tile_by_tile(q_raw, m, q, "q_raw", range(i, i + 1))
                if what == "k":
                    load_tile_by_tile(k_raw, m, k, "k_raw", range(i, i + 1))
                if what == "v":
                    load_whole(v_raw, m, v[(m + 1) % MODS, 0], "v_raw")
                if what == "x":
                    load_whole(x_raw, m, x[m, 0], "x_raw")
                if what == "w":
                    load_weights(m)

        def scores_and_transposes(a, first_scores):
            next_q, key_tile, u_e, u_x = a + 1, a + TILES, a - 2, a - 3
            filled = {}
            if 0 <= next_q < UNITS:
                filled["q"] = psum.tile([P, WORD_CHUNKS, P], F32, name="q_psum", tag="bank")
                q_words = q_raw[next_q // TILES][:, next_q % TILES, :].bitcast(F32)
            if 0 <= u_x < UNITS:
                filled["x"] = psum.tile([P, 2 * X_PASSES, P], F32, name="x_psum", tag="bank")
            if a == 0:
                filled["scores"] = first_scores
            if 0 < a < UNITS:
                filled["scores"] = psum.tile([P, S], F32, name="scores", tag="bank")
            if 0 <= a < UNITS:
                q_pairs = qT[a][:].rearrange("p c (r e) -> p c r e", e=2)
                k_pairs = kT[a // TILES][:].rearrange("p i c (r e) -> p i c r e", e=2)
            if 0 <= key_tile < UNITS:
                filled["k"] = psum.tile([P, WORD_CHUNKS, P], F32, name="k_psum", tag="bank")
                k_words = k_raw[key_tile // TILES][:, key_tile % TILES, :].bitcast(F32)
            if 0 <= u_e < UNITS:
                filled["er"] = psum.tile([P, 3, P], F32, name="er_psum", tag="bank")
                e_words = e_rows[u_e][:].bitcast(F32)
                er_sources = [e_words[:, 0:P], e_words[:, P : 2 * P], recip[u_e][:].to_broadcast([P, P])]
            moves = []
            for j in range(WORD_CHUNKS):
                if 0 <= next_q < UNITS:
                    moves.append((filled["q"][:, j, :], q_words[:, P * j : P * (j + 1)]))
                if 0 <= u_x < UNITS:
                    moves.append((filled["x"][:, j, :], x_sorted[u_x][:, j, :]))
            for j in range(WORD_CHUNKS):
                if 0 <= key_tile < UNITS:
                    moves.append((filled["k"][:, j, :], k_words[:, P * j : P * (j + 1)]))
                if j < 3 and 0 <= u_e < UNITS:
                    moves.append((filled["er"][:, j, :], er_sources[j]))
            products = [(c, e) for c in range(WORD_CHUNKS) for e in range(2)] if 0 <= a < UNITS else []
            gaps = len(products) - 1
            placed = 0
            for n, (c, e) in enumerate(products):
                tiles = slice(TILES - 1, TILES) if a == 0 else slice(0, TILES)
                nc.tensor.matmul(
                    out=filled["scores"][:].rearrange("p (i r) -> p i r", r=P)[:, tiles, :],
                    lhsT=q_pairs[:, c, :, e],
                    rhs=k_pairs[:, tiles, c, :, e],
                    start=(n == 0),
                    stop=(n == gaps),
                )
                if n < gaps:
                    upto = (len(moves) * (n + 1) + gaps - 1) // gaps
                    for target, source in moves[placed:upto]:
                        nc.tensor.transpose(target, source, ident_f32[:])
                    placed = upto
            for target, source in moves[placed:]:
                nc.tensor.transpose(target, source, ident_f32[:])
            return filled

        def first_unit():
            q_psum = psum.tile([P, WORD_CHUNKS, P], F32, name="q_psum", tag="bank")
            q_words = q_raw[0][:, 0, :].bitcast(F32)
            for j in range(WORD_CHUNKS):
                nc.tensor.transpose(q_psum[:, j, :], q_words[:, P * j : P * (j + 1)], ident_f32[:])
            queries_leave_psum(0, q_psum)
            for i in range(TILES):
                k_psum = psum.tile([P, WORD_CHUNKS, P], F32, name="k_psum", tag="bank")
                k_words = k_raw[0][:, i, :].bitcast(F32)
                for j in range(WORD_CHUNKS):
                    nc.tensor.transpose(k_psum[:, j, :], k_words[:, P * j : P * (j + 1)], ident_f32[:])
                keys_leave_psum(i, k_psum)
                if i == 1:
                    scores = psum.tile([P, S], F32, name="scores", tag="bank")
                if i > 0:
                    q_pairs = qT[0][:].rearrange("p c (r e) -> p c r e", e=2)
                    k_pairs = kT[0][:].rearrange("p i c (r e) -> p i c r e", e=2)
                    for c in range(WORD_CHUNKS):
                        for e in range(2):
                            nc.tensor.matmul(
                                out=scores[:, P * (i - 1) : P * i],
                                lhsT=q_pairs[:, c, :, e],
                                rhs=k_pairs[:, i - 1, c, :, e],
                                start=(c == 0 and e == 0),
                                stop=(c == WORD_CHUNKS - 1 and e == 1),
                            )
            return scores

        def queries_leave_psum(u, q_psum):
            qT[u] = work.tile([P, WORD_CHUNKS, 2 * P], BF16, name="qT", tag="qT")
            nc.scalar.copy(out=qT[u][:].bitcast(F32), in_=q_psum[:])

        def e_and_reciprocal_leave_psum(u, er_psum):
            e_grouped = work.tile([P, P * PACK], BF16, name="e_grouped", tag="e_grouped", align_bytes=256)
            nc.scalar.copy(
                out=e_grouped[:].bitcast(F32).rearrange("p (r w) -> p r w", w=2),
                in_=er_psum[:, 0:2, :].rearrange("p w r -> p r w"),
            )
            recip_bc[u] = work.tile([P, P], F32, name="recip_bc", tag="recip_bc")
            nc.scalar.copy(out=recip_bc[u][:], in_=er_psum[:, 2, :])
            return e_grouped

        def quantise_e(u, e_grouped):
            e_codes[u] = work.tile([P, P], U32, name="e_codes", tag="e_codes", align_bytes=256)
            e_plane[u] = work.tile([P, P], U8, name="e_plane", tag="e_plane", align_bytes=256)
            nc.vector.quantize_mx(out=e_codes[u][:].bitcast(FP8X4), scales=e_plane[u][:], in_=e_grouped[:])

        def keys_leave_psum(key_tile, k_psum):
            m, i = key_tile // TILES, key_tile % TILES
            if i == 0:
                kT[m] = work.tile([P, TILES, WORD_CHUNKS, 2 * P], BF16, name="kT", tag="kT")
            nc.scalar.copy(out=kT[m][:, i, :, :].bitcast(F32), in_=k_psum[:])


        def softmax_maximum(a, scores):
            row_max[a] = work.tile([P, 1], F32, name="row_max", tag="row_max")
            nc.vector.tensor_reduce(out=row_max[a][:], in_=scores[:], axis=AXIS.X, op=ALU.max)

        def softmax_exponential(a, scores):
            neg_max = work.tile([P, 1], F32, name="neg_max", tag="neg_max")
            nc.scalar.mul(out=neg_max[:], in_=row_max[a][:], mul=-SCALE)
            e_rows[a] = work.tile([P, S], BF16, name="e_rows", tag="e_rows", bufs=3)
            row_sum[a] = work.tile([P, 1], F32, name="row_sum", tag="row_sum")
            nc.scalar.activation(
                out=e_rows[a][:].rearrange("r (w p e) -> r w p e", w=2, e=2),
                in_=scores[:].rearrange("r (w e p) -> r w p e", w=2, e=2),
                func=ACT.Exp,
                bias=neg_max[:],
                scale=SCALE,
                accum_out=row_sum[a][:],
            )

        def reciprocal(a):
            recip[a] = work.tile([P, 1], F32, name="recip", tag="recip", bufs=3)
            nc.vector.reciprocal(out=recip[a][:], in_=row_sum[a][:])

        def regroup_values(m, g):
            if g == 0:
                v_grouped[m] = work.tile([P, X_PASSES, HALF * PACK], BF16, name="v_grouped", tag="v_grouped", align_bytes=256)
            nc.vector.tensor_copy(
                out=v_grouped[m][:, g, :].rearrange("p (t r j) -> p r j t", t=PACK, j=PACK),
                in_=v_raw[m][:, :, HALF * g : HALF * (g + 1)].rearrange("p j (r t) -> p r j t", t=PACK),
            )

        def quantise_values(m):
            v_codes[m] = work.tile([P, D], U32, name="v_codes", tag="v_codes", align_bytes=256)
            v_plane[m] = work.tile([P, D], U8, name="v_plane", tag="v_plane", align_bytes=256)
            nc.vector.quantize_mx(
                out=v_codes[m][:].bitcast(FP8X4),
                scales=v_plane[m][:],
                in_=v_grouped[m][:].rearrange("p g c -> p (g c)"),
            )

        def sort_x(u):
            words = x_raw[u // TILES][:, u % TILES, :].bitcast(F32)
            x_sorted[u] = work.tile([P, 2 * X_PASSES, P], F32, name="x_sorted", tag="x_sorted", bufs=3)
            nc.scalar.copy(
                out=x_sorted[u][:].rearrange("r (g w) p -> r g w p", w=2),
                in_=words.rearrange("r (g p w) -> r g w p", g=X_PASSES, w=2),
            )

        def x_leaves_psum(u, x_psum):
            comb_grouped[u] = work.tile([P, PASSES, P * PACK], BF16, name="comb_grouped", tag="comb_grouped", align_bytes=256)
            nc.scalar.copy(
                out=comb_grouped[u][:, 0:X_PASSES, :].bitcast(F32).rearrange("p g (r w) -> p g r w", w=2),
                in_=x_psum[:].rearrange("p (g w) r -> p g r w", w=2),
            )

        def context_products(u):
            m = u // TILES
            ctx_psum[u] = []
            for g in range(X_PASSES):
                bank = psum.tile([P, PACK, P], F32, name="ctx_psum", tag="bank")
                for t in range(PACK):
                    cols = slice(P * (PACK * g + t), P * (PACK * g + t + 1))
                    nc.tensor.matmul_mx(
                        out=bank[:, t, :],
                        lhsT=v_codes[m][:, cols].bitcast(FP8X4),
                        lhsT_scale=v_plane[m][:, cols],
                        rhs=e_codes[u][:].bitcast(FP8X4),
                        rhs_scale=e_plane[u][:],
                        start=True,
                        stop=True,
                    )
                ctx_psum[u].append(bank)

        def normalise_context(u):
            for g in range(X_PASSES):
                nc.vector.tensor_tensor(
                    out=comb_grouped[u][:, X_PASSES + g, :].rearrange("p (r t) -> p r t", t=PACK),
                    in0=ctx_psum[u][g][:].rearrange("p t r -> p r t"),
                    in1=recip_bc[u][:].unsqueeze(2).to_broadcast([P, P, PACK]),
                    op=ALU.mult,
                )

        def quantise_concatenation(u):
            comb_codes[u] = work.tile([P, PASSES * P], U32, name="comb_codes", tag="comb_codes", align_bytes=256)
            comb_plane[u] = work.tile([P, PASSES * P], U8, name="comb_plane", tag="comb_plane", align_bytes=256)
            nc.vector.quantize_mx(
                out=comb_codes[u][:].bitcast(FP8X4),
                scales=comb_plane[u][:],
                in_=comb_grouped[u][:].rearrange("p g c -> p (g c)"),
            )

        def output_products(u):
            m = u // TILES
            banks = []
            for h in range(D // HALF):
                banks.append(psum.tile([P, HALF], F32, name="out_psum", tag="bank"))
                for g in range(PASSES):
                    nc.tensor.matmul_mx(
                        out=banks[h][:],
                        lhsT=comb_codes[u][:, P * g : P * (g + 1)].bitcast(FP8X4),
                        lhsT_scale=comb_plane[u][:, P * g : P * (g + 1)],
                        rhs=wo_words[m][:, g, HALF * h : HALF * (h + 1)].bitcast(FP8X4),
                        rhs_scale=wo_planes[4 * g : P, m, HALF * h : HALF * (h + 1)],
                        start=(g == 0),
                        stop=(g == PASSES - 1),
                    )
            return banks

        def add_bias_and_store(u, banks):
            m, i = u // TILES, u % TILES
            for h in range(D // HALF):
                cols = slice(HALF * h, HALF * (h + 1))
                result = work.tile([P, HALF], F32, name="result", tag="result", bufs=6)
                nc.vector.tensor_tensor(out=result[:], in0=banks[h][:], in1=bias[m][:, cols], op=ALU.add)
                nc.sync.dma_start(out=rows_on_partitions(out[m, 0])[:, i, cols], in_=result[:])

        with tc.manual_schedule():
            issue_loads(-1)
            first_scores = first_unit()
            for step in range(0, UNITS + 4):
                u_scores, u_e, u_ctx, u_out = step, step - 2, step - 3, step - 4
                issue_loads(step)
                filled = scores_and_transposes(u_scores, first_scores)
                if "q" in filled:
                    queries_leave_psum(u_scores + 1, filled["q"])
                if "x" in filled:
                    x_leaves_psum(u_ctx, filled["x"])
                if "scores" in filled:
                    softmax_maximum(u_scores, filled["scores"])
                if "scores" in filled and u_scores % TILES < X_PASSES:
                    regroup_values(u_scores // TILES, u_scores % TILES)
                if "scores" in filled and u_scores % TILES == X_PASSES:
                    quantise_values(u_scores // TILES)
                if "er" in filled:
                    e_grouped = e_and_reciprocal_leave_psum(u_e, filled["er"])
                if "k" in filled:
                    keys_leave_psum(u_scores + TILES, filled["k"])
                if "scores" in filled:
                    softmax_exponential(u_scores, filled["scores"])
                if 0 <= u_ctx + 2 < UNITS:
                    sort_x(u_ctx + 2)
                if "er" in filled:
                    quantise_e(u_e, e_grouped)
                if 0 <= u_ctx < UNITS:
                    context_products(u_ctx)
                    normalise_context(u_ctx)
                if "scores" in filled:
                    reciprocal(u_scores)
                if 0 <= u_ctx < UNITS:
                    quantise_concatenation(u_ctx)
                if 0 <= u_out < UNITS:
                    out_banks = output_products(u_out)
                    add_bias_and_store(u_out, out_banks)
